import numpy as np
import ml_dtypes


def mxq(x, axis, fmt="e4m3"):
    dtype, down = {"e4m3": (ml_dtypes.float8_e4m3fn, 7), "e5m2": (ml_dtypes.float8_e5m2, 14)}[fmt]
    v = np.moveaxis(np.asarray(x, np.float32).astype(ml_dtypes.bfloat16).astype(np.float64), axis, -1)
    blocks = v.reshape(v.shape[:-1] + (-1, 32))
    amax = np.abs(blocks).max(-1, keepdims=True)
    byte = np.maximum(np.where(amax > 0, np.frexp(amax)[1] - 1 + 127, 0) - down, 1)
    scale = np.exp2(byte - 127.0)
    codes = (blocks / scale).astype(np.float32).astype(dtype).astype(np.float64)
    return np.moveaxis((codes * scale).reshape(v.shape), -1, axis)


WIDE = False


def mx_kscale(k):
    if not WIDE:
        return np.ones(k)
    levels = np.array([10, -10, 5, -5, 0])
    a = np.random.permutation(np.resize(levels, k // 512 * 4)).reshape(k // 512, 4)
    idx = np.arange(k)
    return np.exp2(a[idx // 512, idx % 128 // 32])


BF16 = ml_dtypes.bfloat16


def bf(x):
    return np.asarray(x, np.float32).astype(BF16)


def f64(x):
    return np.asarray(x).astype(np.float64)


B, K, DIM = 5120, 1024, 512


def setup_inputs():
    t = mx_kscale(DIM)
    t = t / t.min()
    x = np.random.standard_normal((B, DIM)) * 1.2 / DIM ** 0.25
    centers = np.random.uniform(size=(K, DIM)) * 1.6 / DIM ** 0.25
    D = 0.6 * np.random.uniform(size=(K, DIM)) + 0.7
    sign = np.where(np.random.uniform(size=(K, DIM)) < 0.25, -1.0, 1.0)
    return {"x": bf(x * t), "centers": bf(centers * t), "D": bf(D * sign * t * t)}


def reference(x, centers, D):
    x, centers, D = f64(x), f64(centers), f64(D)
    D_abs = np.abs(D) + 1e-4
    D_inv = 1.0 / D_abs
    log_det = np.sum(np.log(D_abs), axis=1)
    det_scale_factor = -0.5 * log_det
    det_scale_safe = np.exp(det_scale_factor - np.max(det_scale_factor))
    x2 = mxq(x * x, 1, "e4m3") @ mxq(D_inv, 1, "e4m3").T
    xc = mxq(x, 1, "e4m3") @ mxq(centers * D_inv, 1, "e4m3").T
    c2 = np.sum(centers * centers * D_inv, axis=1)
    dist_sq = x2 - 2.0 * xc + c2[None, :]
    expo = -0.5 * dist_sq
    expo_safe = expo - np.max(expo, axis=-1, keepdims=True)
    numer_safe = det_scale_safe[None, :] * np.exp(expo_safe)
    denom_safe = np.sum(numer_safe, axis=1, keepdims=True)
    resp = numer_safe / denom_safe
    return resp

@@ -1,0 +1,261 @@
+from contextlib import ExitStack
+
+import concourse.mybir as mybir
+from concourse.masks import make_identity
+
+F32 = mybir.dt.float32
+BF16 = mybir.dt.bfloat16
+I32 = mybir.dt.int32
+U32 = mybir.dt.uint32
+U8 = mybir.dt.uint8
+FP8X4 = mybir.dt.float8_e4m3fn_x4
+ALU = mybir.AluOpType
+ACT = mybir.ActivationFunctionType
+AX = mybir.AxisListType
+
+P = 128
+ROWS = 5120
+CLS = 1024
+DIM = 512
+NT = ROWS // P
+NB = NT // 4
+CT = CLS // P
+HC = CLS // 2
+EPS = 1e-4
+
+FLOPS = 2 * 2 * ROWS * CLS * DIM
+
+
+def tile_axis_aligned_gmm_layer_t_kernel(tc, x, centers, D, out):
+    nc = tc.nc
+    with ExitStack() as ctx:
+        const = ctx.enter_context(tc.tile_pool(name="const", bufs=1))
+        small = ctx.enter_context(tc.tile_pool(name="small", bufs=4))
+        xgp = ctx.enter_context(tc.tile_pool(name="xgp", bufs=2))
+        xqp = ctx.enter_context(tc.tile_pool(name="xqp", bufs=4))
+        work = ctx.enter_context(tc.tile_pool(name="work", bufs=5))
+        ps = ctx.enter_context(tc.psum_pool(name="ps", bufs=8))
+
+        def bank(nm):
+            return ps.tile([P, 512], F32, name=nm, tag="bank")
+
+        one = const.tile([P, 1], F32, name="one", tag="one")
+        nc.vector.memset(one[:], 1.0)
+        warm = const.tile([P, 1], F32, name="warm", tag="warm")
+        nc.scalar.activation(out=warm[:], in_=one[:], func=ACT.Ln)
+        ident = const.tile([P, P], F32, name="ident", tag="ident")
+        make_identity(nc, ident[:])
+        neg_half = const.tile([P, P], F32, name="neg_half", tag="neg_half")
+        nc.vector.memset(neg_half[:], -0.5)
+
+        d_sb = const.tile([P, CT * DIM], BF16, name="d_sb", tag="d_sb")
+        c_sb = const.tile([P, CT * DIM], BF16, name="c_sb", tag="c_sb")
+        x_sb = const.tile([P, NT * DIM], BF16, name="x_sb", tag="x_sb")
+        d_v = D.rearrange("(j p) d -> p j d", p=P)
+        c_v = centers.rearrange("(j p) d -> p j d", p=P)
+        x_v = x.rearrange("(p t) d -> p t d", t=NT)
+        out_v = out.rearrange("(p t) k -> p t k", t=NT)
+        for h in range(2):
+            cols = slice(h * 4 * DIM, (h + 1) * 4 * DIM)
+            nc.sync.dma_start(
+                out=d_sb[:, cols].rearrange("p (j d) -> p j d", j=4), in_=d_v[:, 4 * h : 4 * h + 4, :]
+            )
+            nc.sync.dma_start(
+                out=c_sb[:, cols].rearrange("p (j d) -> p j d", j=4), in_=c_v[:, 4 * h : 4 * h + 4, :]
+            )
+        for c in range(5):
+            nc.sync.dma_start(
+                out=x_sb[:, c * 8 * DIM : (c + 1) * 8 * DIM].rearrange("p (t d) -> p t d", t=8),
+                in_=x_v[:, 8 * c : 8 * c + 8, :],
+            )
+        d_i = d_sb[:].bitcast(I32)
+        d_w = d_sb[:].bitcast(F32)
+        c_w = c_sb[:].bitcast(F32)
+        x_w = x_sb[:].bitcast(F32)
+
+        cg = const.tile([P, CLS * 4], BF16, name="cg", tag="cg")
+        cg_w = cg[:].bitcast(F32)
+        w1g = const.tile([P, CLS * 4], BF16, name="w1g", tag="w1g", align_bytes=64)
+        w2g = const.tile([P, CLS * 4], BF16, name="w2g", tag="w2g", align_bytes=64)
+        w1c = const.tile([P, CLS], U32, name="w1c", tag="w1c", align_bytes=64)
+        w2c = const.tile([P, CLS], U32, name="w2c", tag="w2c", align_bytes=64)
+        w1s = const.tile([P, CLS], U8, name="w1s", tag="w1s", align_bytes=64)
+        w2s = const.tile([P, CLS], U8, name="w2s", tag="w2s", align_bytes=64)
+        g_b = const.tile([P, CLS], F32, name="g_b", tag="g_b")
+        a0 = const.tile([P, 1], F32, name="a0", tag="a0")
+        inv = const.tile([P, 1], F32, name="inv", tag="inv")
+        einv = const.tile([P, 1], F32, name="einv", tag="einv")
+        lninv = const.tile([P, 1], F32, name="lninv", tag="lninv")
+        lnr = [const.tile([P, 4 * HC], F32, name="lnr%d" % h, tag="lnr%d" % h) for h in range(2)]
+        dv = [const.tile([P, 4 * HC], F32, name="dv%d" % h, tag="dv%d" % h) for h in range(2)]
+        csq = [const.tile([P, 4 * HC], F32, name="csq%d" % h, tag="csq%d" % h) for h in range(2)]
+
+        d_t = {}
+        for h in range(2):
+            words = slice(h * 1024, (h + 1) * 1024)
+            nc.vector.tensor_single_scalar(
+                out=d_i[:, words], in_=d_i[:, words], scalar=0x7FFF7FFF, op=ALU.bitwise_and
+            )
+            for u in range(2):
+                d_t[(h, u)] = bank("dT%d%d" % (h, u))
+                for jj in range(4):
+                    src = (4 * h + jj) * 256 + u * P
+                    nc.tensor.transpose(
+                        out=d_t[(h, u)][:, jj * P : (jj + 1) * P], in_=d_w[:, src : src + P], identity=ident[:]
+                    )
+            if h == 0:
+                nc.vector.tensor_scalar_add(out=a0[:], in0=d_t[(0, 0)][:].bitcast(BF16)[:, 0:1], scalar1=EPS)
+                nc.vector.reciprocal(out=inv[:], in_=a0[:])
+                nc.vector.tensor_scalar_mul(out=einv[:], in0=inv[:], scalar1=EPS)
+                nc.scalar.activation(out=lninv[:], in_=inv[:], func=ACT.Ln)
+            for pr in range(2):
+                c_t = bank("cT%d%d" % (h, pr))
+                for jj in range(2):
+                    for u in range(2):
+                        src = (4 * h + 2 * pr + jj) * 256 + u * P
+                        dst = (2 * jj + u) * P
+                        nc.tensor.transpose(out=c_t[:, dst : dst + P], in_=c_w[:, src : src + P], identity=ident[:])
+                w0 = (4 * h + 2 * pr) * P * 2
+                nc.vector.tensor_copy(
+                    out=cg_w[:, w0 : w0 + 512].rearrange("p (j r u) -> p j r u", j=2, u=2),
+                    in_=c_t[:].rearrange("p (j u r) -> p j r u", j=2, u=2),
+                )
+
+        for h in range(2):
+            for u in range(2):
+                nc.scalar.activation(
+                    out=lnr[h][:, 2 * u * HC : (2 * u + 2) * HC].rearrange("p (e r) -> p e r", e=2),
+                    in_=d_t[(h, u)][:].bitcast(BF16).rearrange("p (r e) -> p e r", e=2),
+                    func=ACT.Ln,
+                    scale=inv[:, 0:1],
+                    bias=einv[:, 0:1],
+                )
+        for h in range(2):
+            nc.scalar.activation(
+                out=csq[h][:].rearrange("p (t r) -> p t r", t=4),
+                in_=cg[:, h * 4 * HC : (h + 1) * 4 * HC].rearrange("p (r t) -> p t r", t=4),
+                func=ACT.Square,
+            )
+        g_p = [bank("gP%d" % h) for h in range(2)]
+        for h in range(2):
+            for t in range(4):
+                nc.tensor.matmul(
+                    out=g_p[h][:], lhsT=neg_half[:], rhs=lnr[h][:, t * HC : (t + 1) * HC], start=(t == 0), stop=False
+                )
+        for h in range(2):
+            for pc in range(2):
+                rr = slice(pc * 256, (pc + 1) * 256)
+                nc.scalar.activation(
+                    out=dv[h][:].rearrange("p (t r) -> p t r", t=4)[:, :, rr],
+                    in_=lnr[h][:].rearrange("p (t r) -> p t r", t=4)[:, :, rr],
+                    func=ACT.Exp,
+                    scale=-1.0,
+                    bias=lninv[:, 0:1],
+                )
+                gcols = slice((h * HC + pc * 256) * 4, (h * HC + (pc + 1) * 256) * 4)
+                dv_g = dv[h][:].rearrange("p (t r) -> p r t", t=4)[:, rr, :]
+                nc.gpsimd.tensor_scalar(
+                    out=w1g[:, gcols].rearrange("p (r t) -> p r t", t=4),
+                    in0=dv_g,
+                    scalar1=-0.5,
+                    scalar2=0.0,
+                    op0=ALU.mult,
+                    op1=ALU.add,
+                )
+                nc.vector.tensor_tensor(
+                    out=w2g[:, gcols].rearrange("p (r t) -> p r t", t=4),
+                    in0=dv_g,
+                    in1=cg[:, gcols].rearrange("p (r t) -> p r t", t=4),
+                    op=ALU.mult,
+                )
+            hc = slice(h * HC, (h + 1) * HC)
+            hg = slice(h * HC * 4, (h + 1) * HC * 4)
+            nc.vector.quantize_mx(out=w1c[:, hc].bitcast(FP8X4), scales=w1s[:, hc], in_=w1g[:, hg])
+            nc.vector.quantize_mx(out=w2c[:, hc].bitcast(FP8X4), scales=w2s[:, hc], in_=w2g[:, hg])
+        for h in range(2):
+            for t in range(4):
+                tc_ = slice(t * HC, (t + 1) * HC)
+                nc.gpsimd.tensor_tensor(out=csq[h][:, tc_], in0=dv[h][:, tc_], in1=csq[h][:, tc_], op=ALU.mult)
+                nc.tensor.matmul(out=g_p[h][:], lhsT=neg_half[:], rhs=csq[h][:, tc_], start=False, stop=(t == 3))
+            nc.vector.tensor_copy(out=g_b[:, h * HC : (h + 1) * HC], in_=g_p[h][:])
+
+        xq = {}
+        xs = {}
+
+        def prep(b):
+            xg = xgp.tile([P, 2 * 2048], BF16, name="xg", tag="xg", align_bytes=64)
+            xg_w = xg[:].bitcast(F32)
+            for half in range(2):
+                xt = bank("xT")
+                for i in range(2):
+                    t = 4 * b + 2 * half + i
+                    for u in range(2):
+                        dst = (2 * i + u) * P
+                        src = t * 256 + u * P
+                        nc.tensor.transpose(out=xt[:, dst : dst + P], in_=x_w[:, src : src + P], identity=ident[:])
+                nc.scalar.copy(
+                    out=xg_w[:, half * 512 : (half + 1) * 512].rearrange("p (i r u) -> p i r u", i=2, u=2),
+                    in_=xt[:].rearrange("p (i u r) -> p i r u", i=2, u=2),
+                )
+            nc.scalar.activation(out=xg[:, 2048:4096], in_=xg[:, 0:2048], func=ACT.Square)
+            xq[b] = xqp.tile([P, 1024], U32, name="xq", tag="xq", align_bytes=64)
+            xs[b] = xqp.tile([P, 1024], U8, name="xs", tag="xs", align_bytes=64)
+            nc.vector.quantize_mx(out=xq[b][:].bitcast(FP8X4), scales=xs[b][:], in_=xg[:])
+
+        def pair(tp):
+            s2 = work.tile([P, 2 * CLS], F32, name="s2", tag="s2")
+            for i in range(2):
+                t = 2 * tp + i
+                b = t // 4
+                r0 = (t % 4) * P
+                for h in range(2):
+                    hc = slice(h * HC, (h + 1) * HC)
+                    acc = bank("acc")
+                    nc.tensor.matmul_mx(
+                        out=acc[:],
+                        lhsT=xq[b][:, 512 + r0 : 512 + r0 + P].bitcast(FP8X4),
+                        lhsT_scale=xs[b][:, 512 + r0 : 512 + r0 + P],
+                        rhs=w1c[:, hc].bitcast(FP8X4),
+                        rhs_scale=w1s[:, hc],
+                        start=True,
+                        stop=False,
+                    )
+                    nc.tensor.matmul_mx(
+                        out=acc[:],
+                        lhsT=xq[b][:, r0 : r0 + P].bitcast(FP8X4),
+                        lhsT_scale=xs[b][:, r0 : r0 + P],
+                        rhs=w2c[:, hc].bitcast(FP8X4),
+                        rhs_scale=w2s[:, hc],
+                        start=False,
+                        stop=True,
+                    )
+                    nc.vector.tensor_tensor(
+                        out=s2[:, i * CLS + h * HC : i * CLS + (h + 1) * HC], in0=acc[:], in1=g_b[:, hc], op=ALU.add
+                    )
+            nmax = small.tile([P, 2], F32, name="nmax", tag="nmax")
+            nc.vector.tensor_reduce(
+                out=nmax[:], in_=s2[:].rearrange("p (i k) -> p i k", i=2), axis=AX.X, op=ALU.max, negate=True
+            )
+            sums = small.tile([P, 2], F32, name="sums", tag="sums")
+            for i in range(2):
+                ic = slice(i * CLS, (i + 1) * CLS)
+                nc.scalar.activation(
+                    out=s2[:, ic], in_=s2[:, ic], func=ACT.Exp, bias=nmax[:, i : i + 1], scale=1.0,
+                    accum_out=sums[:, i : i + 1],
+                )
+            rec = small.tile([P, 2], F32, name="rec", tag="rec")
+            nc.vector.reciprocal(out=rec[:], in_=sums[:])
+            for i in range(2):
+                ic = slice(i * CLS, (i + 1) * CLS)
+                nc.gpsimd.tensor_scalar(
+                    out=s2[:, ic], in0=s2[:, ic], scalar1=rec[:, i : i + 1], scalar2=0.0, op0=ALU.mult, op1=ALU.add
+                )
+            nc.sync.dma_start(out=out_v[:, 2 * tp : 2 * tp + 2, :], in_=s2[:].rearrange("p (i k) -> p i k", i=2))
+
+        prep(0)
+        prep(1)
+        for b in range(NB):
+            if b + 2 < NB:
+                prep(b + 2)
+            pair(2 * b)
+            pair(2 * b + 1)

@@ -24,20 +24,31 @@ HC = CLS // 2
 EPS = 1e-4
 
 FLOPS = 2 * 2 * ROWS * CLS * DIM
+PIN = True
+XG_BUFS = 4
+XQ_BUFS = 7
+O4_BUFS = 4
+ST_BUFS = 3
+PRE = 4
+OFF = {"xtr":-16,"xcp":-15,"xq0":-12,"xsq":-13,"xq1":-9,"mt":-6,"md":-6,"ev":-5,"ad":-5,"bt":-1,"em":0,"ex":0,"rc":1,"sc":3}
+SQE = "GG"
+N_LO = -16
+N_HI = 3
 
 
 def tile_axis_aligned_gmm_layer_t_kernel(tc, x, centers, D, out):
     nc = tc.nc
     with ExitStack() as ctx:
+        if PIN:
+            ctx.enter_context(tc.manual_schedule())
         const = ctx.enter_context(tc.tile_pool(name="const", bufs=1))
-        small = ctx.enter_context(tc.tile_pool(name="small", bufs=4))
-        xgp = ctx.enter_context(tc.tile_pool(name="xgp", bufs=2))
-        xqp = ctx.enter_context(tc.tile_pool(name="xqp", bufs=4))
-        work = ctx.enter_context(tc.tile_pool(name="work", bufs=5))
-        ps = ctx.enter_context(tc.psum_pool(name="ps", bufs=8))
+        small = ctx.enter_context(tc.tile_pool(name="small", bufs=6))
+        xgp = ctx.enter_context(tc.tile_pool(name="xgp", bufs=XG_BUFS))
+        xqp = ctx.enter_context(tc.tile_pool(name="xqp", bufs=XQ_BUFS))
+        ps = ctx.enter_context(tc.psum_pool(name="ps", bufs=2))
 
-        def bank(nm):
-            return ps.tile([P, 512], F32, name=nm, tag="bank")
+        def bank(nm, tag):
+            return ps.tile([P, 512], F32, name=nm, tag=tag)
 
         one = const.tile([P, 1], F32, name="one", tag="one")
         nc.vector.memset(one[:], 1.0)
@@ -45,84 +56,121 @@ def tile_axis_aligned_gmm_layer_t_kernel(tc, x, centers, D, out):
         nc.scalar.activation(out=warm[:], in_=one[:], func=ACT.Ln)
         ident = const.tile([P, P], F32, name="ident", tag="ident")
         make_identity(nc, ident[:])
-        neg_half = const.tile([P, P], F32, name="neg_half", tag="neg_half")
-        nc.vector.memset(neg_half[:], -0.5)
+        half_c = const.tile([P, P], F32, name="half_c", tag="half_c")
+        nc.vector.memset(half_c[:], 0.5)
 
-        d_sb = const.tile([P, CT * DIM], BF16, name="d_sb", tag="d_sb")
-        c_sb = const.tile([P, CT * DIM], BF16, name="c_sb", tag="c_sb")
         x_sb = const.tile([P, NT * DIM], BF16, name="x_sb", tag="x_sb")
-        d_v = D.rearrange("(j p) d -> p j d", p=P)
-        c_v = centers.rearrange("(j p) d -> p j d", p=P)
-        x_v = x.rearrange("(p t) d -> p t d", t=NT)
-        out_v = out.rearrange("(p t) k -> p t k", t=NT)
-        for h in range(2):
-            cols = slice(h * 4 * DIM, (h + 1) * 4 * DIM)
-            nc.sync.dma_start(
-                out=d_sb[:, cols].rearrange("p (j d) -> p j d", j=4), in_=d_v[:, 4 * h : 4 * h + 4, :]
-            )
-            nc.sync.dma_start(
-                out=c_sb[:, cols].rearrange("p (j d) -> p j d", j=4), in_=c_v[:, 4 * h : 4 * h + 4, :]
-            )
-        for c in range(5):
-            nc.sync.dma_start(
-                out=x_sb[:, c * 8 * DIM : (c + 1) * 8 * DIM].rearrange("p (t d) -> p t d", t=8),
-                in_=x_v[:, 8 * c : 8 * c + 8, :],
-            )
-        d_i = d_sb[:].bitcast(I32)
-        d_w = d_sb[:].bitcast(F32)
-        c_w = c_sb[:].bitcast(F32)
-        x_w = x_sb[:].bitcast(F32)
-
-        cg = const.tile([P, CLS * 4], BF16, name="cg", tag="cg")
-        cg_w = cg[:].bitcast(F32)
-        w1g = const.tile([P, CLS * 4], BF16, name="w1g", tag="w1g", align_bytes=64)
-        w2g = const.tile([P, CLS * 4], BF16, name="w2g", tag="w2g", align_bytes=64)
         w1c = const.tile([P, CLS], U32, name="w1c", tag="w1c", align_bytes=64)
         w2c = const.tile([P, CLS], U32, name="w2c", tag="w2c", align_bytes=64)
         w1s = const.tile([P, CLS], U8, name="w1s", tag="w1s", align_bytes=64)
         w2s = const.tile([P, CLS], U8, name="w2s", tag="w2s", align_bytes=64)
         g_b = const.tile([P, CLS], F32, name="g_b", tag="g_b")
+        gcol = const.tile([P, 4], F32, name="gcol", tag="gcol")
         a0 = const.tile([P, 1], F32, name="a0", tag="a0")
         inv = const.tile([P, 1], F32, name="inv", tag="inv")
         einv = const.tile([P, 1], F32, name="einv", tag="einv")
         lninv = const.tile([P, 1], F32, name="lninv", tag="lninv")
-        lnr = [const.tile([P, 4 * HC], F32, name="lnr%d" % h, tag="lnr%d" % h) for h in range(2)]
-        dv = [const.tile([P, 4 * HC], F32, name="dv%d" % h, tag="dv%d" % h) for h in range(2)]
-        csq = [const.tile([P, 4 * HC], F32, name="csq%d" % h, tag="csq%d" % h) for h in range(2)]
+        x_w = x_sb[:].bitcast(F32)
+        x_v = x.rearrange("(p t) d -> p t d", t=NT)
+        out_v = out.rearrange("(p t) k -> p t k", t=NT)
+        d_v = D.rearrange("(j p) d -> p j d", p=P)
+        c_v = centers.rearrange("(j p) d -> p j d", p=P)
 
-        d_t = {}
-        for h in range(2):
-            words = slice(h * 1024, (h + 1) * 1024)
-            nc.vector.tensor_single_scalar(
-                out=d_i[:, words], in_=d_i[:, words], scalar=0x7FFF7FFF, op=ALU.bitwise_and
-            )
-            for u in range(2):
-                d_t[(h, u)] = bank("dT%d%d" % (h, u))
-                for jj in range(4):
-                    src = (4 * h + jj) * 256 + u * P
+        xg = {}
+        xt = {}
+        xq = {}
+        xs = {}
+
+        def x_tr(b, half):
+            if half == 0:
+                xg[b] = xgp.tile([P, 2 * 2048], BF16, name="xg", tag="xg", align_bytes=64)
+                xq[b] = xqp.tile([P, 1024], U32, name="xq", tag="xq", align_bytes=64)
+                xs[b] = xqp.tile([P, 1024], U8, name="xs", tag="xs", align_bytes=64)
+            xt[(b, half)] = bank("xT", "pd")
+            for i in range(2):
+                t = 4 * b + 2 * half + i
+                for u in range(2):
+                    dst = (2 * i + u) * P
+                    src = t * 256 + u * P
                     nc.tensor.transpose(
-                        out=d_t[(h, u)][:, jj * P : (jj + 1) * P], in_=d_w[:, src : src + P], identity=ident[:]
+                        out=xt[(b, half)][:, dst : dst + P], in_=x_w[:, src : src + P], identity=ident[:]
                     )
-            if h == 0:
+
+        def x_cp(b, half, eng):
+            o_ap = xg[b][:].bitcast(F32)[:, half * 512 : (half + 1) * 512].rearrange("p (i r u) -> p i r u", i=2, u=2)
+            i_ap = xt[(b, half)][:].rearrange("p (i u r) -> p i r u", i=2, u=2)
+            if eng == "V":
+                nc.vector.tensor_copy(out=o_ap, in_=i_ap)
+            else:
+                nc.scalar.copy(out=o_ap, in_=i_ap)
+
+        def x_sq(b, z, eng):
+            zi = slice(z * 1024, (z + 1) * 1024)
+            zo = slice(2048 + z * 1024, 2048 + (z + 1) * 1024)
+            if eng == "S":
+                nc.scalar.activation(out=xg[b][:, zo], in_=xg[b][:, zi], func=ACT.Square)
+            elif eng == "V":
+                nc.vector.tensor_tensor(out=xg[b][:, zo], in0=xg[b][:, zi], in1=xg[b][:, zi], op=ALU.mult)
+            else:
+                nc.gpsimd.tensor_tensor(out=xg[b][:, zo], in0=xg[b][:, zi], in1=xg[b][:, zi], op=ALU.mult)
+
+        def x_qt(b, kind):
+            nc.vector.quantize_mx(
+                out=xq[b][:, kind * 512 : (kind + 1) * 512].bitcast(FP8X4),
+                scales=xs[b][:, kind * 512 : (kind + 1) * 512],
+                in_=xg[b][:, kind * 2048 : (kind + 1) * 2048],
+            )
+
+        with tc.tile_pool(name="pro", bufs=1) as pro:
+            d_sb = pro.tile([P, CT * DIM], BF16, name="d_sb", tag="d_sb")
+            c_sb = pro.tile([P, CT * DIM], BF16, name="c_sb", tag="c_sb")
+            for src_v, dst_t in ((d_v, d_sb), (c_v, c_sb)):
+                for h in range(2):
+                    cols = slice(h * 4 * DIM, (h + 1) * 4 * DIM)
+                    nc.sync.dma_start(
+                        out=dst_t[:, cols].rearrange("p (j d) -> p j d", j=4), in_=src_v[:, 4 * h : 4 * h + 4, :]
+                    )
+            for c in range(5):
+                nc.sync.dma_start(
+                    out=x_sb[:, c * 8 * DIM : (c + 1) * 8 * DIM].rearrange("p (t d) -> p t d", t=8),
+                    in_=x_v[:, 8 * c : 8 * c + 8, :],
+                )
+            d_i = d_sb[:].bitcast(I32)
+            d_w = d_sb[:].bitcast(F32)
+            c_w = c_sb[:].bitcast(F32)
+            cg = pro.tile([P, CLS * 4], BF16, name="cg", tag="cg")
+            cg_w = cg[:].bitcast(F32)
+            w1g = pro.tile([P, CLS * 4], BF16, name="w1g", tag="w1g", align_bytes=64)
+            w2g = pro.tile([P, CLS * 4], BF16, name="w2g", tag="w2g", align_bytes=64)
+            lnr = [pro.tile([P, 4 * HC], F32, name="lnr%d" % h, tag="lnr%d" % h) for h in range(2)]
+            dv = [pro.tile([P, 4 * HC], F32, name="dv%d" % h, tag="dv%d" % h) for h in range(2)]
+            csq = [pro.tile([P, 4 * HC], F32, name="csq%d" % h, tag="csq%d" % h) for h in range(2)]
+            d_t = {}
+            c_t = {}
+            g_p = {}
+
+            def p_and(h):
+                words = slice(h * 1024, (h + 1) * 1024)
+                nc.vector.tensor_single_scalar(
+                    out=d_i[:, words], in_=d_i[:, words], scalar=0x7FFF7FFF, op=ALU.bitwise_and
+                )
+
+            def p_dtr(h):
+                for u in range(2):
+                    d_t[(h, u)] = bank("dT", "pa" if h == 0 else "pb")
+                    for jj in range(4):
+                        src = (4 * h + jj) * 256 + u * P
+                        nc.tensor.transpose(
+                            out=d_t[(h, u)][:, jj * P : (jj + 1) * P], in_=d_w[:, src : src + P], identity=ident[:]
+                        )
+
+            def p_rho():
                 nc.vector.tensor_scalar_add(out=a0[:], in0=d_t[(0, 0)][:].bitcast(BF16)[:, 0:1], scalar1=EPS)
                 nc.vector.reciprocal(out=inv[:], in_=a0[:])
                 nc.vector.tensor_scalar_mul(out=einv[:], in0=inv[:], scalar1=EPS)
                 nc.scalar.activation(out=lninv[:], in_=inv[:], func=ACT.Ln)
-            for pr in range(2):
-                c_t = bank("cT%d%d" % (h, pr))
-                for jj in range(2):
-                    for u in range(2):
-                        src = (4 * h + 2 * pr + jj) * 256 + u * P
-                        dst = (2 * jj + u) * P
-                        nc.tensor.transpose(out=c_t[:, dst : dst + P], in_=c_w[:, src : src + P], identity=ident[:])
-                w0 = (4 * h + 2 * pr) * P * 2
-                nc.vector.tensor_copy(
-                    out=cg_w[:, w0 : w0 + 512].rearrange("p (j r u) -> p j r u", j=2, u=2),
-                    in_=c_t[:].rearrange("p (j u r) -> p j r u", j=2, u=2),
-                )
 
-        for h in range(2):
-            for u in range(2):
+            def p_ln(h, u):
                 nc.scalar.activation(
                     out=lnr[h][:, 2 * u * HC : (2 * u + 2) * HC].rearrange("p (e r) -> p e r", e=2),
                     in_=d_t[(h, u)][:].bitcast(BF16).rearrange("p (r e) -> p e r", e=2),
@@ -130,20 +178,42 @@ def tile_axis_aligned_gmm_layer_t_kernel(tc, x, centers, D, out):
                     scale=inv[:, 0:1],
                     bias=einv[:, 0:1],
                 )
-        for h in range(2):
-            nc.scalar.activation(
-                out=csq[h][:].rearrange("p (t r) -> p t r", t=4),
-                in_=cg[:, h * 4 * HC : (h + 1) * 4 * HC].rearrange("p (r t) -> p t r", t=4),
-                func=ACT.Square,
-            )
-        g_p = [bank("gP%d" % h) for h in range(2)]
-        for h in range(2):
-            for t in range(4):
-                nc.tensor.matmul(
-                    out=g_p[h][:], lhsT=neg_half[:], rhs=lnr[h][:, t * HC : (t + 1) * HC], start=(t == 0), stop=False
+
+            def p_ctr(h, pr):
+                c_t[(h, pr)] = bank("cT", "pc" if h == 0 else "pd")
+                for jj in range(2):
+                    for u in range(2):
+                        src = (4 * h + 2 * pr + jj) * 256 + u * P
+                        dst = (2 * jj + u) * P
+                        nc.tensor.transpose(
+                            out=c_t[(h, pr)][:, dst : dst + P], in_=c_w[:, src : src + P], identity=ident[:]
+                        )
+
+            def p_cgc(h, pr):
+                w0 = (4 * h + 2 * pr) * P * 2
+                nc.vector.tensor_copy(
+                    out=cg_w[:, w0 : w0 + 512].rearrange("p (j r u) -> p j r u", j=2, u=2),
+                    in_=c_t[(h, pr)][:].rearrange("p (j u r) -> p j r u", j=2, u=2),
                 )
-        for h in range(2):
-            for pc in range(2):
+
+            def p_csq(h, eng):
+                cg_t = cg[:, h * 4 * HC : (h + 1) * 4 * HC].rearrange("p (r t) -> p t r", t=4)
+                cs_t = csq[h][:].rearrange("p (t r) -> p t r", t=4)
+                if eng == "V":
+                    nc.vector.tensor_tensor(out=cs_t, in0=cg_t, in1=cg_t, op=ALU.mult)
+                elif eng == "S":
+                    nc.scalar.activation(out=cs_t, in_=cg_t, func=ACT.Square)
+                else:
+                    nc.gpsimd.tensor_tensor(out=cs_t, in0=cg_t, in1=cg_t, op=ALU.mult)
+
+            def p_gl(h, t):
+                if t == 0:
+                    g_p[h] = bank("gP", "pa")
+                nc.tensor.matmul(
+                    out=g_p[h][:], lhsT=half_c[:], rhs=lnr[h][:, t * HC : (t + 1) * HC], start=(t == 0), stop=False
+                )
+
+            def p_exp(h, pc):
                 rr = slice(pc * 256, (pc + 1) * 256)
                 nc.scalar.activation(
                     out=dv[h][:].rearrange("p (t r) -> p t r", t=4)[:, :, rr],
@@ -152,110 +222,279 @@ def tile_axis_aligned_gmm_layer_t_kernel(tc, x, centers, D, out):
                     scale=-1.0,
                     bias=lninv[:, 0:1],
                 )
+
+            def p_w1(h, pc, eng):
+                rr = slice(pc * 256, (pc + 1) * 256)
                 gcols = slice((h * HC + pc * 256) * 4, (h * HC + (pc + 1) * 256) * 4)
-                dv_g = dv[h][:].rearrange("p (t r) -> p r t", t=4)[:, rr, :]
-                nc.gpsimd.tensor_scalar(
+                e = nc.gpsimd if eng == "G" else nc.vector
+                e.tensor_scalar(
                     out=w1g[:, gcols].rearrange("p (r t) -> p r t", t=4),
-                    in0=dv_g,
-                    scalar1=-0.5,
+                    in0=dv[h][:].rearrange("p (t r) -> p r t", t=4)[:, rr, :],
+                    scalar1=0.5,
                     scalar2=0.0,
                     op0=ALU.mult,
                     op1=ALU.add,
                 )
-                nc.vector.tensor_tensor(
+
+            def p_w2(h, pc):
+                rr = slice(pc * 256, (pc + 1) * 256)
+                gcols = slice((h * HC + pc * 256) * 4, (h * HC + (pc + 1) * 256) * 4)
+                nc.vector.scalar_tensor_tensor(
                     out=w2g[:, gcols].rearrange("p (r t) -> p r t", t=4),
-                    in0=dv_g,
+                    in0=dv[h][:].rearrange("p (t r) -> p r t", t=4)[:, rr, :],
+                    scalar=-1.0,
                     in1=cg[:, gcols].rearrange("p (r t) -> p r t", t=4),
-                    op=ALU.mult,
+                    op0=ALU.mult,
+                    op1=ALU.mult,
                 )
-            hc = slice(h * HC, (h + 1) * HC)
-            hg = slice(h * HC * 4, (h + 1) * HC * 4)
-            nc.vector.quantize_mx(out=w1c[:, hc].bitcast(FP8X4), scales=w1s[:, hc], in_=w1g[:, hg])
-            nc.vector.quantize_mx(out=w2c[:, hc].bitcast(FP8X4), scales=w2s[:, hc], in_=w2g[:, hg])
-        for h in range(2):
+
+            def p_qw(h, which):
+                hc = slice(h * HC, (h + 1) * HC)
+                hg = slice(h * HC * 4, (h + 1) * HC * 4)
+                if which == 1:
+                    nc.vector.quantize_mx(out=w1c[:, hc].bitcast(FP8X4), scales=w1s[:, hc], in_=w1g[:, hg])
+                else:
+                    nc.vector.quantize_mx(out=w2c[:, hc].bitcast(FP8X4), scales=w2s[:, hc], in_=w2g[:, hg])
+
+            def p_q(h, t, eng):
+                ts = slice(t * HC, (t + 1) * HC)
+                e = nc.gpsimd if eng == "G" else nc.vector
+                e.tensor_tensor(out=csq[h][:, ts], in0=dv[h][:, ts], in1=csq[h][:, ts], op=ALU.mult)
+
+            def p_gq(h, t):
+                ts = slice(t * HC, (t + 1) * HC)
+                nc.tensor.matmul(out=g_p[h][:], lhsT=half_c[:], rhs=csq[h][:, ts], start=False, stop=(t == 3))
+
+            def p_gb(h):
+                nc.scalar.copy(out=g_b[:, h * HC : (h + 1) * HC], in_=g_p[h][:])
+
+            def p_gcol():
+                g_t = bank("gT", "pb")
+                for jj in range(4):
+                    nc.tensor.transpose(
+                        out=g_t[:, jj * P : (jj + 1) * P], in_=g_b[:, jj * P : (jj + 1) * P], identity=ident[:]
+                    )
+                nc.vector.tensor_copy(
+                    out=gcol[:].rearrange("p (j o) -> p j o", o=1),
+                    in_=g_t[:].rearrange("p (j r) -> p j r", j=4)[:, :, 0:1],
+                )
+
+            p_and(0)
+            p_and(1)
+            p_dtr(0)
+            p_rho()
+            p_dtr(1)
+            for h in range(2):
+                for u in range(2):
+                    p_ln(h, u)
+            for h in range(2):
+                for pr in range(2):
+                    p_ctr(h, pr)
+                    p_cgc(h, pr)
+            p_csq(0, "V")
             for t in range(4):
-                tc_ = slice(t * HC, (t + 1) * HC)
-                nc.gpsimd.tensor_tensor(out=csq[h][:, tc_], in0=dv[h][:, tc_], in1=csq[h][:, tc_], op=ALU.mult)
-                nc.tensor.matmul(out=g_p[h][:], lhsT=neg_half[:], rhs=csq[h][:, tc_], start=False, stop=(t == 3))
-            nc.vector.tensor_copy(out=g_b[:, h * HC : (h + 1) * HC], in_=g_p[h][:])
+                p_gl(0, t)
+            x_tr(0, 0)
+            x_tr(0, 1)
+            p_csq(1, "V")
+            for t in range(4):
+                p_gl(1, t)
+            for h in range(2):
+                for pc in range(2):
+                    p_exp(h, pc)
+                    p_w1(h, pc, "G")
+                    p_w2(h, pc)
+                p_qw(h, 2)
+                p_qw(h, 1)
+            x_cp(0, 0, "S")
+            x_cp(0, 1, "S")
+            x_tr(1, 0)
+            x_tr(1, 1)
+            x_sq(0, 0, "S")
+            x_sq(0, 1, "S")
+            x_cp(1, 0, "S")
+            x_cp(1, 1, "S")
+            x_tr(2, 0)
+            x_tr(2, 1)
+            for t in range(4):
+                p_q(1, t, "G")
+                p_q(0, t, "V")
+            for t in range(2):
+                p_gq(1, t)
+                p_gq(0, t)
+            x_sq(1, 0, "S")
+            x_sq(1, 1, "S")
+            x_cp(2, 0, "S")
+            x_cp(2, 1, "S")
+            x_tr(3, 0)
+            x_tr(3, 1)
+            for t in range(2, 4):
+                p_gq(1, t)
+                p_gq(0, t)
+            x_cp(3, 0, "S")
+            x_cp(3, 1, "S")
+            x_sq(2, 0, "G")
+            x_sq(2, 1, "G")
+            x_sq(3, 0, "G")
+            x_sq(3, 1, "G")
+            for b in range(2):
+                x_qt(b, 0)
+                x_qt(b, 1)
+            x_qt(2, 0)
+            x_qt(3, 0)
+            x_qt(2, 1)
+            p_gb(0)
+            p_gcol()
+            p_gb(1)
+            x_qt(3, 1)
 
-        xq = {}
-        xs = {}
+        work = ctx.enter_context(tc.tile_pool(name="work", bufs=O4_BUFS))
+        stp = ctx.enter_context(tc.tile_pool(name="stp", bufs=ST_BUFS))
+        o4 = {}
+        s_t = {}
+        pt = {}
+        acc = {}
+        st = {}
+        dmin = {}
+        nmin = {}
+        sums = {}
+        rec = {}
 
-        def prep(b):
-            xg = xgp.tile([P, 2 * 2048], BF16, name="xg", tag="xg", align_bytes=64)
-            xg_w = xg[:].bitcast(F32)
-            for half in range(2):
-                xt = bank("xT")
-                for i in range(2):
-                    t = 4 * b + 2 * half + i
-                    for u in range(2):
-                        dst = (2 * i + u) * P
-                        src = t * 256 + u * P
-                        nc.tensor.transpose(out=xt[:, dst : dst + P], in_=x_w[:, src : src + P], identity=ident[:])
-                nc.scalar.copy(
-                    out=xg_w[:, half * 512 : (half + 1) * 512].rearrange("p (i r u) -> p i r u", i=2, u=2),
-                    in_=xt[:].rearrange("p (i u r) -> p i r u", i=2, u=2),
-                )
-            nc.scalar.activation(out=xg[:, 2048:4096], in_=xg[:, 0:2048], func=ACT.Square)
-            xq[b] = xqp.tile([P, 1024], U32, name="xq", tag="xq", align_bytes=64)
-            xs[b] = xqp.tile([P, 1024], U8, name="xs", tag="xs", align_bytes=64)
-            nc.vector.quantize_mx(out=xq[b][:].bitcast(FP8X4), scales=xs[b][:], in_=xg[:])
-
-        def pair(tp):
-            s2 = work.tile([P, 2 * CLS], F32, name="s2", tag="s2")
-            for i in range(2):
-                t = 2 * tp + i
-                b = t // 4
-                r0 = (t % 4) * P
-                for h in range(2):
-                    hc = slice(h * HC, (h + 1) * HC)
-                    acc = bank("acc")
-                    nc.tensor.matmul_mx(
-                        out=acc[:],
-                        lhsT=xq[b][:, 512 + r0 : 512 + r0 + P].bitcast(FP8X4),
-                        lhsT_scale=xs[b][:, 512 + r0 : 512 + r0 + P],
-                        rhs=w1c[:, hc].bitcast(FP8X4),
-                        rhs_scale=w1s[:, hc],
-                        start=True,
-                        stop=False,
-                    )
-                    nc.tensor.matmul_mx(
-                        out=acc[:],
-                        lhsT=xq[b][:, r0 : r0 + P].bitcast(FP8X4),
-                        lhsT_scale=xs[b][:, r0 : r0 + P],
-                        rhs=w2c[:, hc].bitcast(FP8X4),
-                        rhs_scale=w2s[:, hc],
-                        start=False,
-                        stop=True,
-                    )
-                    nc.vector.tensor_tensor(
-                        out=s2[:, i * CLS + h * HC : i * CLS + (h + 1) * HC], in0=acc[:], in1=g_b[:, hc], op=ALU.add
-                    )
-            nmax = small.tile([P, 2], F32, name="nmax", tag="nmax")
-            nc.vector.tensor_reduce(
-                out=nmax[:], in_=s2[:].rearrange("p (i k) -> p i k", i=2), axis=AX.X, op=ALU.max, negate=True
+        def mx_pair(dst, l1, l1s, r1, r1s, l2, l2s, r2, r2s):
+            nc.tensor.matmul_mx(
+                out=dst, lhsT=l1.bitcast(FP8X4), lhsT_scale=l1s, rhs=r1.bitcast(FP8X4), rhs_scale=r1s,
+                start=True, stop=False,
             )
-            sums = small.tile([P, 2], F32, name="sums", tag="sums")
-            for i in range(2):
-                ic = slice(i * CLS, (i + 1) * CLS)
-                nc.scalar.activation(
-                    out=s2[:, ic], in_=s2[:, ic], func=ACT.Exp, bias=nmax[:, i : i + 1], scale=1.0,
-                    accum_out=sums[:, i : i + 1],
-                )
-            rec = small.tile([P, 2], F32, name="rec", tag="rec")
-            nc.vector.reciprocal(out=rec[:], in_=sums[:])
-            for i in range(2):
-                ic = slice(i * CLS, (i + 1) * CLS)
-                nc.gpsimd.tensor_scalar(
-                    out=s2[:, ic], in0=s2[:, ic], scalar1=rec[:, i : i + 1], scalar2=0.0, op0=ALU.mult, op1=ALU.add
-                )
-            nc.sync.dma_start(out=out_v[:, 2 * tp : 2 * tp + 2, :], in_=s2[:].rearrange("p (i k) -> p i k", i=2))
+            nc.tensor.matmul_mx(
+                out=dst, lhsT=l2.bitcast(FP8X4), lhsT_scale=l2s, rhs=r2.bitcast(FP8X4), rhs_scale=r2s,
+                start=False, stop=True,
+            )
 
-        prep(0)
-        prep(1)
-        for b in range(NB):
-            if b + 2 < NB:
-                prep(b + 2)
-            pair(2 * b)
-            pair(2 * b + 1)
+        def m_t(b, jj):
+            if jj == 0:
+                s_t[b] = stp.tile([P, 4 * 512], F32, name="s_t", tag="s_t")
+            jc = slice(jj * P, (jj + 1) * P)
+            pt[(b, jj)] = bank("pt", "pb")
+            mx_pair(
+                pt[(b, jj)][:], w1c[:, jc], w1s[:, jc], xq[b][:, 512:1024], xs[b][:, 512:1024],
+                w2c[:, jc], w2s[:, jc], xq[b][:, 0:512], xs[b][:, 0:512],
+            )
+
+        def e_v(b, jj, eng):
+            if eng == "S":
+                nc.scalar.activation(
+                    out=s_t[b][:, jj * 512 : (jj + 1) * 512], in_=pt[(b, jj)][:], func=ACT.Identity,
+                    bias=gcol[:, jj : jj + 1], scale=1.0,
+                )
+            else:
+                nc.vector.tensor_scalar_add(
+                    out=s_t[b][:, jj * 512 : (jj + 1) * 512], in0=pt[(b, jj)][:], scalar1=gcol[:, jj : jj + 1]
+                )
+
+        def m_d(b, i):
+            if i == 0:
+                o4[b] = work.tile([P, 4 * CLS], F32, name="o4", tag="o4")
+            rc = slice(i * P, (i + 1) * P)
+            rc2 = slice(512 + i * P, 512 + (i + 1) * P)
+            hc = slice(HC, CLS)
+            acc[(b, i)] = bank("acc", "pc")
+            mx_pair(
+                acc[(b, i)][:], xq[b][:, rc2], xs[b][:, rc2], w1c[:, hc], w1s[:, hc],
+                xq[b][:, rc], xs[b][:, rc], w2c[:, hc], w2s[:, hc],
+            )
+
+        def a_d(b, i):
+            nc.vector.tensor_tensor(
+                out=o4[b][:, i * CLS + HC : (i + 1) * CLS], in0=acc[(b, i)][:], in1=g_b[:, HC:CLS], op=ALU.add
+            )
+
+        def d_m(b):
+            dmin[b] = small.tile([P, 4], F32, name="dmin", tag="dmin")
+            nmin[b] = small.tile([P, 4], F32, name="nmin", tag="nmin")
+            nc.vector.tensor_reduce(
+                out=dmin[b][:], in_=o4[b][:].rearrange("p (i k) -> p i k", i=4)[:, :, HC:CLS], axis=AX.X, op=ALU.min
+            )
+
+        def b_t(b, i):
+            st[(b, i)] = bank("st", "pa")
+            for jj in range(4):
+                nc.tensor.transpose(
+                    out=st[(b, i)][:, jj * P : (jj + 1) * P],
+                    in_=s_t[b][:, jj * 512 + i * P : jj * 512 + (i + 1) * P],
+                    identity=ident[:],
+                )
+
+        def e_m(b, i):
+            nc.vector.tensor_scalar(
+                out=o4[b][:, i * CLS : i * CLS + HC], in0=st[(b, i)][:], scalar1=0.0, scalar2=dmin[b][:, i : i + 1],
+                op0=ALU.add, op1=ALU.min, accum_out=nmin[b][:, i : i + 1],
+            )
+
+        def e_x(b, i):
+            if i % 2 == 0:
+                sums[(b, i // 2)] = small.tile([P, 2], F32, name="sums", tag="sums")
+            ic = slice(i * CLS, (i + 1) * CLS)
+            nc.scalar.activation(
+                out=o4[b][:, ic], in_=o4[b][:, ic], func=ACT.Exp, bias=nmin[b][:, i : i + 1], scale=-1.0,
+                accum_out=sums[(b, i // 2)][:, i % 2 : i % 2 + 1],
+            )
+
+        def r_c(b, pr):
+            rec[(b, pr)] = small.tile([P, 2], F32, name="rec", tag="rec")
+            nc.vector.reciprocal(out=rec[(b, pr)][:], in_=sums[(b, pr)][:])
+
+        def s_c(b, i):
+            ic = slice(i * CLS, (i + 1) * CLS)
+            nc.gpsimd.tensor_scalar(
+                out=o4[b][:, ic], in0=o4[b][:, ic], scalar1=rec[(b, i // 2)][:, i % 2 : i % 2 + 1], scalar2=0.0,
+                op0=ALU.mult, op1=ALU.add,
+            )
+
+        def s_t_ore(b, pr):
+            t0 = 4 * b + 2 * pr
+            nc.sync.dma_start(
+                out=out_v[:, t0 : t0 + 2, :],
+                in_=o4[b][:].rearrange("p (i k) -> p i k", i=4)[:, 2 * pr : 2 * pr + 2, :],
+            )
+
+        def sched(n):
+            todo = {}
+            for key in OFF:
+                m = n - OFF[key]
+                todo[key] = (m // 4, m % 4) if 0 <= m < 4 * NB else None
+            return todo
+
+        for n in range(N_LO, 4 * NB + N_HI + 1):
+            td = sched(n)
+            if td["bt"]:
+                b_t(*td["bt"])
+            if td["xtr"] and td["xtr"][1] % 2 == 0 and td["xtr"][0] >= PRE:
+                x_tr(td["xtr"][0], td["xtr"][1] // 2)
+            if td["mt"]:
+                m_t(*td["mt"])
+            if td["md"]:
+                m_d(*td["md"])
+            if td["em"]:
+                e_m(*td["em"])
+            if td["ev"]:
+                e_v(td["ev"][0], td["ev"][1], "S")
+            if td["ad"]:
+                a_d(*td["ad"])
+                if td["ad"][1] == 3:
+                    d_m(td["ad"][0])
+            if td["ex"]:
+                e_x(*td["ex"])
+            if td["xcp"] and td["xcp"][1] % 2 == 0 and td["xcp"][0] >= PRE:
+                x_cp(td["xcp"][0], td["xcp"][1] // 2, "S")
+            if td["xq0"] and td["xq0"][1] == 0 and td["xq0"][0] >= PRE:
+                x_qt(td["xq0"][0], 0)
+            if td["rc"] and td["rc"][1] % 2 == 1:
+                r_c(td["rc"][0], td["rc"][1] // 2)
+            if td["sc"]:
+                s_c(*td["sc"])
+                if td["sc"][1] % 2 == 1:
+                    s_t_ore(td["sc"][0], td["sc"][1] // 2)
+            if td["xsq"] and td["xsq"][1] % 2 == 0 and td["xsq"][0] >= PRE:
+                x_sq(td["xsq"][0], td["xsq"][1] // 2, SQE[td["xsq"][1] // 2])
+            if td["xq1"] and td["xq1"][1] == 0 and td["xq1"][0] >= PRE:
+                x_qt(td["xq1"][0], 1)

@@ -31,7 +31,7 @@ O4_BUFS = 4
 ST_BUFS = 3
 PRE = 4
 OFF = {"xtr":-16,"xcp":-15,"xq0":-12,"xsq":-13,"xq1":-9,"mt":-6,"md":-6,"ev":-5,"ad":-5,"bt":-1,"em":0,"ex":0,"rc":1,"sc":3}
-SQE = "GG"
+SQE = "VS"
 N_LO = -16
 N_HI = 3
 

@@ -31,9 +31,12 @@ O4_BUFS = 4
 ST_BUFS = 3
 PRE = 4
 OFF = {"xtr":-16,"xcp":-15,"xq0":-12,"xsq":-13,"xq1":-9,"mt":-6,"md":-6,"ev":-5,"ad":-5,"bt":-1,"em":0,"ex":0,"rc":1,"sc":3}
-SQE = "VS"
+SQE = "VG"
 N_LO = -16
 N_HI = 3
+PRE_Q1 = 2
+LASTV = 1
+SQM = ["","","","","VG","VG","VG","VG","VG","VG"]
 
 
 def tile_axis_aligned_gmm_layer_t_kernel(tc, x, centers, D, out):
@@ -279,6 +282,76 @@ def tile_axis_aligned_gmm_layer_t_kernel(tc, x, centers, D, out):
                     in_=g_t[:].rearrange("p (j r) -> p j r", j=4)[:, :, 0:1],
                 )
 
+            glcol = pro.tile([P, 4], F32, name="glcol", tag="glcol")
+            gl_b = pro.tile([P, HC], F32, name="gl_b", tag="gl_b")
+            c2col = [pro.tile([P, 4], F32, name="c2col%d" % h, tag="c2col%d" % h) for h in range(2)]
+            c2h = pro.tile([P, 4], F32, name="c2h", tag="c2h")
+            q_a = {}
+
+            def p_gl2(h, t):
+                if t == 0:
+                    g_p[h] = bank("gP", "pa")
+                nc.tensor.matmul(
+                    out=g_p[h][:], lhsT=half_c[:], rhs=lnr[h][:, t * HC : (t + 1) * HC], start=(t == 0), stop=(t == 3)
+                )
+
+            def p_glc():
+                nc.scalar.copy(out=g_b[:, 0:HC], in_=g_p[0][:])
+                g_t = bank("gT", "pa")
+                for jj in range(4):
+                    nc.tensor.transpose(
+                        out=g_t[:, jj * P : (jj + 1) * P], in_=g_b[:, jj * P : (jj + 1) * P], identity=ident[:]
+                    )
+                nc.scalar.copy(
+                    out=glcol[:].rearrange("p (j o) -> p j o", o=1),
+                    in_=g_t[:].rearrange("p (j r) -> p j r", j=4)[:, :, 0:1],
+                )
+
+            def p_glb():
+                nc.scalar.copy(out=gl_b[:], in_=g_p[1][:])
+
+            def p_qp(h, pc, eng):
+                rr = slice(pc * 256, (pc + 1) * 256)
+                e = nc.gpsimd if eng == "G" else nc.vector
+                e.tensor_tensor(
+                    out=csq[h][:].rearrange("p (t r) -> p t r", t=4)[:, :, rr],
+                    in0=dv[h][:].rearrange("p (t r) -> p t r", t=4)[:, :, rr],
+                    in1=csq[h][:].rearrange("p (t r) -> p t r", t=4)[:, :, rr],
+                    op=ALU.mult,
+                )
+
+            def p_at(h, jj, tag):
+                if jj == 0:
+                    q_a[h] = bank("qA", tag)
+                for t in range(4):
+                    nc.tensor.matmul(
+                        out=q_a[h][:, jj * P : (jj + 1) * P],
+                        lhsT=csq[h][:, t * HC + jj * P : t * HC + (jj + 1) * P],
+                        rhs=ident[:],
+                        is_transpose=True,
+                        start=(t == 0),
+                        stop=(t == 3),
+                    )
+
+            def p_c2(h):
+                nc.vector.tensor_reduce(
+                    out=c2col[h][:], in_=q_a[h][:].rearrange("p (j r) -> p j r", j=4), axis=AX.X, op=ALU.add
+                )
+                if h == 0:
+                    nc.vector.scalar_tensor_tensor(
+                        out=gcol[:], in0=c2col[0][:], scalar=0.5, in1=glcol[:], op0=ALU.mult, op1=ALU.add
+                    )
+                else:
+                    nc.vector.tensor_scalar_mul(out=c2h[:], in0=c2col[1][:], scalar1=0.5)
+
+            def p_gb2(tag):
+                b_b = bank("bB", tag)
+                for jj in range(4):
+                    nc.tensor.transpose(
+                        out=b_b[:, jj * P : (jj + 1) * P], in_=c2h[:, jj : jj + 1].to_broadcast([P, P]), identity=ident[:]
+                    )
+                nc.vector.tensor_tensor(out=g_b[:, HC:CLS], in0=b_b[:], in1=gl_b[:], op=ALU.add)
+
             p_and(0)
             p_and(1)
             p_dtr(0)
@@ -291,62 +364,62 @@ def tile_axis_aligned_gmm_layer_t_kernel(tc, x, centers, D, out):
                 for pr in range(2):
                     p_ctr(h, pr)
                     p_cgc(h, pr)
-            p_csq(0, "V")
-            for t in range(4):
-                p_gl(0, t)
+                p_csq(h, "G")
             x_tr(0, 0)
             x_tr(0, 1)
-            p_csq(1, "V")
             for t in range(4):
-                p_gl(1, t)
+                p_gl2(0, t)
+            x_cp(0, 0, "V")
+            x_cp(0, 1, "V")
+            x_qt(0, 0)
+            x_sq(0, 0, "V")
+            x_sq(0, 1, "V")
+            x_qt(0, 1)
+            x_tr(1, 0)
+            x_tr(1, 1)
+            for t in range(4):
+                p_gl2(1, t)
             for h in range(2):
                 for pc in range(2):
                     p_exp(h, pc)
-                    p_w1(h, pc, "G")
+                    p_w1(h, pc, "V")
                     p_w2(h, pc)
                 p_qw(h, 2)
                 p_qw(h, 1)
-            x_cp(0, 0, "S")
-            x_cp(0, 1, "S")
-            x_tr(1, 0)
-            x_tr(1, 1)
-            x_sq(0, 0, "S")
-            x_sq(0, 1, "S")
+                if h == 0:
+                    p_qp(0, 0, "V")
+                    p_qp(0, 1, "V")
+            p_glc()
+            p_glb()
+            for jj in range(4):
+                p_at(0, jj, "pc")
+            p_qp(1, 0, "G")
+            p_qp(1, 1, "G")
             x_cp(1, 0, "S")
             x_cp(1, 1, "S")
             x_tr(2, 0)
             x_tr(2, 1)
-            for t in range(4):
-                p_q(1, t, "G")
-                p_q(0, t, "V")
-            for t in range(2):
-                p_gq(1, t)
-                p_gq(0, t)
+            p_c2(0)
             x_sq(1, 0, "S")
             x_sq(1, 1, "S")
             x_cp(2, 0, "S")
             x_cp(2, 1, "S")
+            for jj in range(4):
+                p_at(1, jj, "pc")
+            x_qt(1, 0)
+            p_c2(1)
+            p_gb2("pc")
             x_tr(3, 0)
             x_tr(3, 1)
-            for t in range(2, 4):
-                p_gq(1, t)
-                p_gq(0, t)
+            x_sq(2, 0, "S")
+            x_sq(2, 1, "G")
             x_cp(3, 0, "S")
             x_cp(3, 1, "S")
-            x_sq(2, 0, "G")
-            x_sq(2, 1, "G")
             x_sq(3, 0, "G")
             x_sq(3, 1, "G")
-            for b in range(2):
-                x_qt(b, 0)
-                x_qt(b, 1)
+            x_qt(1, 1)
             x_qt(2, 0)
             x_qt(3, 0)
-            x_qt(2, 1)
-            p_gb(0)
-            p_gcol()
-            p_gb(1)
-            x_qt(3, 1)
 
         work = ctx.enter_context(tc.tile_pool(name="work", bufs=O4_BUFS))
         stp = ctx.enter_context(tc.tile_pool(name="stp", bufs=ST_BUFS))
@@ -443,12 +516,27 @@ def tile_axis_aligned_gmm_layer_t_kernel(tc, x, centers, D, out):
             rec[(b, pr)] = small.tile([P, 2], F32, name="rec", tag="rec")
             nc.vector.reciprocal(out=rec[(b, pr)][:], in_=sums[(b, pr)][:])
 
-        def s_c(b, i):
-            ic = slice(i * CLS, (i + 1) * CLS)
-            nc.gpsimd.tensor_scalar(
-                out=o4[b][:, ic], in0=o4[b][:, ic], scalar1=rec[(b, i // 2)][:, i % 2 : i % 2 + 1], scalar2=0.0,
-                op0=ALU.mult, op1=ALU.add,
+        def r_c1(b, i):
+            if i % 2 == 0:
+                rec[(b, i // 2)] = small.tile([P, 2], F32, name="rec", tag="rec")
+            nc.vector.reciprocal(
+                out=rec[(b, i // 2)][:, i % 2 : i % 2 + 1], in_=sums[(b, i // 2)][:, i % 2 : i % 2 + 1]
             )
+
+        def s_c(b, i, eng="G"):
+            ic = slice(i * CLS, (i + 1) * CLS)
+            if eng == "V":
+                nc.vector.tensor_scalar_mul(
+                    out=o4[b][:, ic], in0=o4[b][:, ic], scalar1=rec[(b, i // 2)][:, i % 2 : i % 2 + 1]
+                )
+            else:
+                nc.gpsimd.tensor_scalar(
+                    out=o4[b][:, ic], in0=o4[b][:, ic], scalar1=rec[(b, i // 2)][:, i % 2 : i % 2 + 1], scalar2=0.0,
+                    op0=ALU.mult, op1=ALU.add,
+                )
+
+        def store1(b, i):
+            nc.sync.dma_start(out=out_v[:, 4 * b + i, :], in_=o4[b][:, i * CLS : (i + 1) * CLS])
 
         def s_t_ore(b, pr):
             t0 = 4 * b + 2 * pr
@@ -488,13 +576,17 @@ def tile_axis_aligned_gmm_layer_t_kernel(tc, x, centers, D, out):
                 x_cp(td["xcp"][0], td["xcp"][1] // 2, "S")
             if td["xq0"] and td["xq0"][1] == 0 and td["xq0"][0] >= PRE:
                 x_qt(td["xq0"][0], 0)
-            if td["rc"] and td["rc"][1] % 2 == 1:
+            if td["rc"] and td["rc"][0] >= NB - LASTV:
+                r_c1(*td["rc"])
+                s_c(td["rc"][0], td["rc"][1], "V")
+                store1(*td["rc"])
+            elif td["rc"] and td["rc"][1] % 2 == 1:
                 r_c(td["rc"][0], td["rc"][1] // 2)
-            if td["sc"]:
+            if td["sc"] and td["sc"][0] < NB - LASTV:
                 s_c(*td["sc"])
                 if td["sc"][1] % 2 == 1:
                     s_t_ore(td["sc"][0], td["sc"][1] // 2)
             if td["xsq"] and td["xsq"][1] % 2 == 0 and td["xsq"][0] >= PRE:
-                x_sq(td["xsq"][0], td["xsq"][1] // 2, SQE[td["xsq"][1] // 2])
-            if td["xq1"] and td["xq1"][1] == 0 and td["xq1"][0] >= PRE:
+                x_sq(td["xsq"][0], td["xsq"][1] // 2, SQM[td["xsq"][0]][td["xsq"][1] // 2])
+            if td["xq1"] and td["xq1"][1] == 0 and td["xq1"][0] >= PRE_Q1:
                 x_qt(td["xq1"][0], 1)

@@ -30,13 +30,14 @@ XQ_BUFS = 7
 O4_BUFS = 4
 ST_BUFS = 3
 PRE = 4
-OFF = {"xtr":-16,"xcp":-15,"xq0":-12,"xsq":-13,"xq1":-9,"mt":-6,"md":-6,"ev":-5,"ad":-5,"bt":-1,"em":0,"ex":0,"rc":1,"sc":3}
+OFF = {"xtr":-16,"xcp":-15,"xq0":-12,"xsq":-13,"xq1":-9,"mt":-6,"md":-6,"ev":-5,"ad":-5,"bt":-1,"em":0,"ex":0,"rc":1,"sc":4}
 SQE = "VG"
 N_LO = -16
-N_HI = 3
+N_HI = 4
 PRE_Q1 = 2
 LASTV = 1
-SQM = ["","","","","VG","VG","VG","VG","VG","VG"]
+SQM = ["","","","","SG","VG","SG","VG","SG","VG"]
+LAST1 = 2
 
 
 def tile_axis_aligned_gmm_layer_t_kernel(tc, x, centers, D, out):
@@ -229,6 +230,14 @@ def tile_axis_aligned_gmm_layer_t_kernel(tc, x, centers, D, out):
             def p_w1(h, pc, eng):
                 rr = slice(pc * 256, (pc + 1) * 256)
                 gcols = slice((h * HC + pc * 256) * 4, (h * HC + (pc + 1) * 256) * 4)
+                if eng == "S":
+                    nc.scalar.activation(
+                        out=w1g[:, gcols].rearrange("p (r t) -> p r t", t=4),
+                        in_=dv[h][:].rearrange("p (t r) -> p r t", t=4)[:, rr, :],
+                        func=ACT.Copy,
+                        scale=0.5,
+                    )
+                    return
                 e = nc.gpsimd if eng == "G" else nc.vector
                 e.tensor_scalar(
                     out=w1g[:, gcols].rearrange("p (r t) -> p r t", t=4),
@@ -382,10 +391,8 @@ def tile_axis_aligned_gmm_layer_t_kernel(tc, x, centers, D, out):
             for h in range(2):
                 for pc in range(2):
                     p_exp(h, pc)
-                    p_w1(h, pc, "V")
                     p_w2(h, pc)
                 p_qw(h, 2)
-                p_qw(h, 1)
                 if h == 0:
                     p_qp(0, 0, "V")
                     p_qp(0, 1, "V")
@@ -395,30 +402,35 @@ def tile_axis_aligned_gmm_layer_t_kernel(tc, x, centers, D, out):
                 p_at(0, jj, "pc")
             p_qp(1, 0, "G")
             p_qp(1, 1, "G")
-            x_cp(1, 0, "S")
-            x_cp(1, 1, "S")
+            for h in range(2):
+                for pc in range(2):
+                    p_w1(h, pc, "S")
+            x_cp(1, 0, "V")
+            x_cp(1, 1, "V")
             x_tr(2, 0)
             x_tr(2, 1)
             p_c2(0)
-            x_sq(1, 0, "S")
-            x_sq(1, 1, "S")
+            x_qt(1, 0)
+            x_sq(1, 0, "V")
+            x_sq(1, 1, "V")
+            x_qt(1, 1)
+            p_qw(0, 1)
+            p_qw(1, 1)
             x_cp(2, 0, "S")
             x_cp(2, 1, "S")
             for jj in range(4):
                 p_at(1, jj, "pc")
-            x_qt(1, 0)
-            p_c2(1)
-            p_gb2("pc")
             x_tr(3, 0)
             x_tr(3, 1)
+            x_qt(2, 0)
+            p_c2(1)
+            p_gb2("pc")
             x_sq(2, 0, "S")
             x_sq(2, 1, "G")
             x_cp(3, 0, "S")
             x_cp(3, 1, "S")
             x_sq(3, 0, "G")
             x_sq(3, 1, "G")
-            x_qt(1, 1)
-            x_qt(2, 0)
             x_qt(3, 0)
 
         work = ctx.enter_context(tc.tile_pool(name="work", bufs=O4_BUFS))
@@ -504,34 +516,30 @@ def tile_axis_aligned_gmm_layer_t_kernel(tc, x, centers, D, out):
             )
 
         def e_x(b, i):
-            if i % 2 == 0:
-                sums[(b, i // 2)] = small.tile([P, 2], F32, name="sums", tag="sums")
+            if i == 0:
+                sums[b] = small.tile([P, 4], F32, name="sums", tag="sums")
+                rec[b] = small.tile([P, 4], F32, name="rec", tag="rec")
             ic = slice(i * CLS, (i + 1) * CLS)
             nc.scalar.activation(
                 out=o4[b][:, ic], in_=o4[b][:, ic], func=ACT.Exp, bias=nmin[b][:, i : i + 1], scale=-1.0,
-                accum_out=sums[(b, i // 2)][:, i % 2 : i % 2 + 1],
+                accum_out=sums[b][:, i : i + 1],
             )
 
-        def r_c(b, pr):
-            rec[(b, pr)] = small.tile([P, 2], F32, name="rec", tag="rec")
-            nc.vector.reciprocal(out=rec[(b, pr)][:], in_=sums[(b, pr)][:])
+        def r_c(b):
+            nc.vector.reciprocal(out=rec[b][:], in_=sums[b][:])
 
         def r_c1(b, i):
-            if i % 2 == 0:
-                rec[(b, i // 2)] = small.tile([P, 2], F32, name="rec", tag="rec")
-            nc.vector.reciprocal(
-                out=rec[(b, i // 2)][:, i % 2 : i % 2 + 1], in_=sums[(b, i // 2)][:, i % 2 : i % 2 + 1]
-            )
+            nc.vector.reciprocal(out=rec[b][:, i : i + 1], in_=sums[b][:, i : i + 1])
 
         def s_c(b, i, eng="G"):
             ic = slice(i * CLS, (i + 1) * CLS)
             if eng == "V":
                 nc.vector.tensor_scalar_mul(
-                    out=o4[b][:, ic], in0=o4[b][:, ic], scalar1=rec[(b, i // 2)][:, i % 2 : i % 2 + 1]
+                    out=o4[b][:, ic], in0=o4[b][:, ic], scalar1=rec[b][:, i : i + 1]
                 )
             else:
                 nc.gpsimd.tensor_scalar(
-                    out=o4[b][:, ic], in0=o4[b][:, ic], scalar1=rec[(b, i // 2)][:, i % 2 : i % 2 + 1], scalar2=0.0,
+                    out=o4[b][:, ic], in0=o4[b][:, ic], scalar1=rec[b][:, i : i + 1], scalar2=0.0,
                     op0=ALU.mult, op1=ALU.add,
                 )
 
@@ -580,11 +588,13 @@ def tile_axis_aligned_gmm_layer_t_kernel(tc, x, centers, D, out):
                 r_c1(*td["rc"])
                 s_c(td["rc"][0], td["rc"][1], "V")
                 store1(*td["rc"])
-            elif td["rc"] and td["rc"][1] % 2 == 1:
-                r_c(td["rc"][0], td["rc"][1] // 2)
+            elif td["rc"] and td["rc"][1] == 3:
+                r_c(td["rc"][0])
             if td["sc"] and td["sc"][0] < NB - LASTV:
                 s_c(*td["sc"])
-                if td["sc"][1] % 2 == 1:
+                if td["sc"][0] >= NB - LAST1:
+                    store1(*td["sc"])
+                elif td["sc"][1] % 2 == 1:
                     s_t_ore(td["sc"][0], td["sc"][1] // 2)
             if td["xsq"] and td["xsq"][1] % 2 == 0 and td["xsq"][0] >= PRE:
                 x_sq(td["xsq"][0], td["xsq"][1] // 2, SQM[td["xsq"][0]][td["xsq"][1] // 2])

@@ -373,64 +373,62 @@ def tile_axis_aligned_gmm_layer_t_kernel(tc, x, centers, D, out):
                 for pr in range(2):
                     p_ctr(h, pr)
                     p_cgc(h, pr)
-                p_csq(h, "G")
-            x_tr(0, 0)
-            x_tr(0, 1)
+            p_csq(0, "V")
             for t in range(4):
                 p_gl2(0, t)
-            x_cp(0, 0, "V")
-            x_cp(0, 1, "V")
-            x_qt(0, 0)
-            x_sq(0, 0, "V")
-            x_sq(0, 1, "V")
-            x_qt(0, 1)
-            x_tr(1, 0)
-            x_tr(1, 1)
+            x_tr(0, 0)
+            x_tr(0, 1)
+            p_csq(1, "V")
             for t in range(4):
                 p_gl2(1, t)
             for h in range(2):
                 for pc in range(2):
                     p_exp(h, pc)
+                    p_w1(h, pc, "G")
                     p_w2(h, pc)
                 p_qw(h, 2)
                 if h == 0:
                     p_qp(0, 0, "V")
                     p_qp(0, 1, "V")
+                p_qw(h, 1)
             p_glc()
             p_glb()
             for jj in range(4):
                 p_at(0, jj, "pc")
-            p_qp(1, 0, "G")
-            p_qp(1, 1, "G")
-            for h in range(2):
-                for pc in range(2):
-                    p_w1(h, pc, "S")
-            x_cp(1, 0, "V")
-            x_cp(1, 1, "V")
-            x_tr(2, 0)
-            x_tr(2, 1)
+            p_qp(1, 0, "V")
+            p_qp(1, 1, "V")
+            x_cp(0, 0, "S")
+            x_cp(0, 1, "S")
+            x_tr(1, 0)
+            x_tr(1, 1)
             p_c2(0)
-            x_qt(1, 0)
-            x_sq(1, 0, "V")
-            x_sq(1, 1, "V")
-            x_qt(1, 1)
-            p_qw(0, 1)
-            p_qw(1, 1)
-            x_cp(2, 0, "S")
-            x_cp(2, 1, "S")
+            x_sq(0, 0, "S")
+            x_sq(0, 1, "S")
+            x_cp(1, 0, "S")
+            x_cp(1, 1, "S")
             for jj in range(4):
                 p_at(1, jj, "pc")
-            x_tr(3, 0)
-            x_tr(3, 1)
-            x_qt(2, 0)
+            x_qt(0, 0)
             p_c2(1)
             p_gb2("pc")
-            x_sq(2, 0, "S")
-            x_sq(2, 1, "G")
+            x_tr(2, 0)
+            x_tr(2, 1)
+            x_sq(1, 0, "S")
+            x_sq(1, 1, "S")
+            x_cp(2, 0, "S")
+            x_cp(2, 1, "S")
+            x_tr(3, 0)
+            x_tr(3, 1)
             x_cp(3, 0, "S")
             x_cp(3, 1, "S")
+            x_sq(2, 0, "G")
+            x_sq(2, 1, "G")
             x_sq(3, 0, "G")
             x_sq(3, 1, "G")
+            x_qt(0, 1)
+            x_qt(1, 0)
+            x_qt(1, 1)
+            x_qt(2, 0)
             x_qt(3, 0)
 
         work = ctx.enter_context(tc.tile_pool(name="work", bufs=O4_BUFS))

@@ -390,7 +390,6 @@ def tile_axis_aligned_gmm_layer_t_kernel(tc, x, centers, D, out):
                 if h == 0:
                     p_qp(0, 0, "V")
                     p_qp(0, 1, "V")
-                p_qw(h, 1)
             p_glc()
             p_glb()
             for jj in range(4):
@@ -411,6 +410,8 @@ def tile_axis_aligned_gmm_layer_t_kernel(tc, x, centers, D, out):
             x_qt(0, 0)
             p_c2(1)
             p_gb2("pc")
+            p_qw(0, 1)
+            p_qw(1, 1)
             x_tr(2, 0)
             x_tr(2, 1)
             x_sq(1, 0, "S")

@@ -24,7 +24,7 @@ HC = CLS // 2
 EPS = 1e-4
 
 FLOPS = 2 * 2 * ROWS * CLS * DIM
-PIN = True
+PIN = False
 XG_BUFS = 4
 XQ_BUFS = 7
 O4_BUFS = 4

from contextlib import ExitStack

import concourse.mybir as mybir
from concourse.masks import make_identity

F32 = mybir.dt.float32
BF16 = mybir.dt.bfloat16
I32 = mybir.dt.int32
U32 = mybir.dt.uint32
U8 = mybir.dt.uint8
FP8X4 = mybir.dt.float8_e4m3fn_x4
ALU = mybir.AluOpType
ACT = mybir.ActivationFunctionType
AX = mybir.AxisListType

P = 128
ROWS = 5120
CLS = 1024
DIM = 512
NT = ROWS // P
NB = NT // 4
CT = CLS // P
HC = CLS // 2
EPS = 1e-4

FLOPS = 2 * 2 * ROWS * CLS * DIM
PIN = False
XG_BUFS = 4
XQ_BUFS = 7
O4_BUFS = 4
ST_BUFS = 3
PRE = 4
OFF = {"xtr":-16,"xcp":-15,"xq0":-12,"xsq":-13,"xq1":-9,"mt":-6,"md":-6,"ev":-5,"ad":-5,"bt":-1,"em":0,"ex":0,"rc":1,"sc":4}
SQE = "VG"
N_LO = -16
N_HI = 4
PRE_Q1 = 2
LASTV = 1
SQM = ["","","","","SG","VG","SG","VG","SG","VG"]
LAST1 = 2


def tile_axis_aligned_gmm_layer_t_kernel(tc, x, centers, D, out):
    nc = tc.nc
    with ExitStack() as ctx:
        if PIN:
            ctx.enter_context(tc.manual_schedule())
        const = ctx.enter_context(tc.tile_pool(name="const", bufs=1))
        small = ctx.enter_context(tc.tile_pool(name="small", bufs=6))
        xgp = ctx.enter_context(tc.tile_pool(name="xgp", bufs=XG_BUFS))
        xqp = ctx.enter_context(tc.tile_pool(name="xqp", bufs=XQ_BUFS))
        ps = ctx.enter_context(tc.psum_pool(name="ps", bufs=2))

        def bank(nm, tag):
            return ps.tile([P, 512], F32, name=nm, tag=tag)

        one = const.tile([P, 1], F32, name="one", tag="one")
        nc.vector.memset(one[:], 1.0)
        warm = const.tile([P, 1], F32, name="warm", tag="warm")
        nc.scalar.activation(out=warm[:], in_=one[:], func=ACT.Ln)
        ident = const.tile([P, P], F32, name="ident", tag="ident")
        make_identity(nc, ident[:])
        half_c = const.tile([P, P], F32, name="half_c", tag="half_c")
        nc.vector.memset(half_c[:], 0.5)

        x_sb = const.tile([P, NT * DIM], BF16, name="x_sb", tag="x_sb")
        w1c = const.tile([P, CLS], U32, name="w1c", tag="w1c", align_bytes=64)
        w2c = const.tile([P, CLS], U32, name="w2c", tag="w2c", align_bytes=64)
        w1s = const.tile([P, CLS], U8, name="w1s", tag="w1s", align_bytes=64)
        w2s = const.tile([P, CLS], U8, name="w2s", tag="w2s", align_bytes=64)
        g_b = const.tile([P, CLS], F32, name="g_b", tag="g_b")
        gcol = const.tile([P, 4], F32, name="gcol", tag="gcol")
        a0 = const.tile([P, 1], F32, name="a0", tag="a0")
        inv = const.tile([P, 1], F32, name="inv", tag="inv")
        einv = const.tile([P, 1], F32, name="einv", tag="einv")
        lninv = const.tile([P, 1], F32, name="lninv", tag="lninv")
        x_w = x_sb[:].bitcast(F32)
        x_v = x.rearrange("(p t) d -> p t d", t=NT)
        out_v = out.rearrange("(p t) k -> p t k", t=NT)
        d_v = D.rearrange("(j p) d -> p j d", p=P)
        c_v = centers.rearrange("(j p) d -> p j d", p=P)

        xg = {}
        xt = {}
        xq = {}
        xs = {}

        def x_tr(b, half):
            if half == 0:
                xg[b] = xgp.tile([P, 2 * 2048], BF16, name="xg", tag="xg", align_bytes=64)
                xq[b] = xqp.tile([P, 1024], U32, name="xq", tag="xq", align_bytes=64)
                xs[b] = xqp.tile([P, 1024], U8, name="xs", tag="xs", align_bytes=64)
            xt[(b, half)] = bank("xT", "pd")
            for i in range(2):
                t = 4 * b + 2 * half + i
                for u in range(2):
                    dst = (2 * i + u) * P
                    src = t * 256 + u * P
                    nc.tensor.transpose(
                        out=xt[(b, half)][:, dst : dst + P], in_=x_w[:, src : src + P], identity=ident[:]
                    )

        def x_cp(b, half, eng):
            o_ap = xg[b][:].bitcast(F32)[:, half * 512 : (half + 1) * 512].rearrange("p (i r u) -> p i r u", i=2, u=2)
            i_ap = xt[(b, half)][:].rearrange("p (i u r) -> p i r u", i=2, u=2)
            if eng == "V":
                nc.vector.tensor_copy(out=o_ap, in_=i_ap)
            else:
                nc.scalar.copy(out=o_ap, in_=i_ap)

        def x_sq(b, z, eng):
            zi = slice(z * 1024, (z + 1) * 1024)
            zo = slice(2048 + z * 1024, 2048 + (z + 1) * 1024)
            if eng == "S":
                nc.scalar.activation(out=xg[b][:, zo], in_=xg[b][:, zi], func=ACT.Square)
            elif eng == "V":
                nc.vector.tensor_tensor(out=xg[b][:, zo], in0=xg[b][:, zi], in1=xg[b][:, zi], op=ALU.mult)
            else:
                nc.gpsimd.tensor_tensor(out=xg[b][:, zo], in0=xg[b][:, zi], in1=xg[b][:, zi], op=ALU.mult)

        def x_qt(b, kind):
            nc.vector.quantize_mx(
                out=xq[b][:, kind * 512 : (kind + 1) * 512].bitcast(FP8X4),
                scales=xs[b][:, kind * 512 : (kind + 1) * 512],
                in_=xg[b][:, kind * 2048 : (kind + 1) * 2048],
            )

        with tc.tile_pool(name="pro", bufs=1) as pro:
            d_sb = pro.tile([P, CT * DIM], BF16, name="d_sb", tag="d_sb")
            c_sb = pro.tile([P, CT * DIM], BF16, name="c_sb", tag="c_sb")
            for src_v, dst_t in ((d_v, d_sb), (c_v, c_sb)):
                for h in range(2):
                    cols = slice(h * 4 * DIM, (h + 1) * 4 * DIM)
                    nc.sync.dma_start(
                        out=dst_t[:, cols].rearrange("p (j d) -> p j d", j=4), in_=src_v[:, 4 * h : 4 * h + 4, :]
                    )
            for c in range(5):
                nc.sync.dma_start(
                    out=x_sb[:, c * 8 * DIM : (c + 1) * 8 * DIM].rearrange("p (t d) -> p t d", t=8),
                    in_=x_v[:, 8 * c : 8 * c + 8, :],
                )
            d_i = d_sb[:].bitcast(I32)
            d_w = d_sb[:].bitcast(F32)
            c_w = c_sb[:].bitcast(F32)
            cg = pro.tile([P, CLS * 4], BF16, name="cg", tag="cg")
            cg_w = cg[:].bitcast(F32)
            w1g = pro.tile([P, CLS * 4], BF16, name="w1g", tag="w1g", align_bytes=64)
            w2g = pro.tile([P, CLS * 4], BF16, name="w2g", tag="w2g", align_bytes=64)
            lnr = [pro.tile([P, 4 * HC], F32, name="lnr%d" % h, tag="lnr%d" % h) for h in range(2)]
            dv = [pro.tile([P, 4 * HC], F32, name="dv%d" % h, tag="dv%d" % h) for h in range(2)]
            csq = [pro.tile([P, 4 * HC], F32, name="csq%d" % h, tag="csq%d" % h) for h in range(2)]
            d_t = {}
            c_t = {}
            g_p = {}

            def p_and(h):
                words = slice(h * 1024, (h + 1) * 1024)
                nc.vector.tensor_single_scalar(
                    out=d_i[:, words], in_=d_i[:, words], scalar=0x7FFF7FFF, op=ALU.bitwise_and
                )

            def p_dtr(h):
                for u in range(2):
                    d_t[(h, u)] = bank("dT", "pa" if h == 0 else "pb")
                    for jj in range(4):
                        src = (4 * h + jj) * 256 + u * P
                        nc.tensor.transpose(
                            out=d_t[(h, u)][:, jj * P : (jj + 1) * P], in_=d_w[:, src : src + P], identity=ident[:]
                        )

            def p_rho():
                nc.vector.tensor_scalar_add(out=a0[:], in0=d_t[(0, 0)][:].bitcast(BF16)[:, 0:1], scalar1=EPS)
                nc.vector.reciprocal(out=inv[:], in_=a0[:])
                nc.vector.tensor_scalar_mul(out=einv[:], in0=inv[:], scalar1=EPS)
                nc.scalar.activation(out=lninv[:], in_=inv[:], func=ACT.Ln)

            def p_ln(h, u):
                nc.scalar.activation(
                    out=lnr[h][:, 2 * u * HC : (2 * u + 2) * HC].rearrange("p (e r) -> p e r", e=2),
                    in_=d_t[(h, u)][:].bitcast(BF16).rearrange("p (r e) -> p e r", e=2),
                    func=ACT.Ln,
                    scale=inv[:, 0:1],
                    bias=einv[:, 0:1],
                )

            def p_ctr(h, pr):
                c_t[(h, pr)] = bank("cT", "pc" if h == 0 else "pd")
                for jj in range(2):
                    for u in range(2):
                        src = (4 * h + 2 * pr + jj) * 256 + u * P
                        dst = (2 * jj + u) * P
                        nc.tensor.transpose(
                            out=c_t[(h, pr)][:, dst : dst + P], in_=c_w[:, src : src + P], identity=ident[:]
                        )

            def p_cgc(h, pr):
                w0 = (4 * h + 2 * pr) * P * 2
                nc.vector.tensor_copy(
                    out=cg_w[:, w0 : w0 + 512].rearrange("p (j r u) -> p j r u", j=2, u=2),
                    in_=c_t[(h, pr)][:].rearrange("p (j u r) -> p j r u", j=2, u=2),
                )

            def p_csq(h, eng):
                cg_t = cg[:, h * 4 * HC : (h + 1) * 4 * HC].rearrange("p (r t) -> p t r", t=4)
                cs_t = csq[h][:].rearrange("p (t r) -> p t r", t=4)
                if eng == "V":
                    nc.vector.tensor_tensor(out=cs_t, in0=cg_t, in1=cg_t, op=ALU.mult)
                elif eng == "S":
                    nc.scalar.activation(out=cs_t, in_=cg_t, func=ACT.Square)
                else:
                    nc.gpsimd.tensor_tensor(out=cs_t, in0=cg_t, in1=cg_t, op=ALU.mult)

            def p_gl(h, t):
                if t == 0:
                    g_p[h] = bank("gP", "pa")
                nc.tensor.matmul(
                    out=g_p[h][:], lhsT=half_c[:], rhs=lnr[h][:, t * HC : (t + 1) * HC], start=(t == 0), stop=False
                )

            def p_exp(h, pc):
                rr = slice(pc * 256, (pc + 1) * 256)
                nc.scalar.activation(
                    out=dv[h][:].rearrange("p (t r) -> p t r", t=4)[:, :, rr],
                    in_=lnr[h][:].rearrange("p (t r) -> p t r", t=4)[:, :, rr],
                    func=ACT.Exp,
                    scale=-1.0,
                    bias=lninv[:, 0:1],
                )

            def p_w1(h, pc, eng):
                rr = slice(pc * 256, (pc + 1) * 256)
                gcols = slice((h * HC + pc * 256) * 4, (h * HC + (pc + 1) * 256) * 4)
                if eng == "S":
                    nc.scalar.activation(
                        out=w1g[:, gcols].rearrange("p (r t) -> p r t", t=4),
                        in_=dv[h][:].rearrange("p (t r) -> p r t", t=4)[:, rr, :],
                        func=ACT.Copy,
                        scale=0.5,
                    )
                    return
                e = nc.gpsimd if eng == "G" else nc.vector
                e.tensor_scalar(
                    out=w1g[:, gcols].rearrange("p (r t) -> p r t", t=4),
                    in0=dv[h][:].rearrange("p (t r) -> p r t", t=4)[:, rr, :],
                    scalar1=0.5,
                    scalar2=0.0,
                    op0=ALU.mult,
                    op1=ALU.add,
                )

            def p_w2(h, pc):
                rr = slice(pc * 256, (pc + 1) * 256)
                gcols = slice((h * HC + pc * 256) * 4, (h * HC + (pc + 1) * 256) * 4)
                nc.vector.scalar_tensor_tensor(
                    out=w2g[:, gcols].rearrange("p (r t) -> p r t", t=4),
                    in0=dv[h][:].rearrange("p (t r) -> p r t", t=4)[:, rr, :],
                    scalar=-1.0,
                    in1=cg[:, gcols].rearrange("p (r t) -> p r t", t=4),
                    op0=ALU.mult,
                    op1=ALU.mult,
                )

            def p_qw(h, which):
                hc = slice(h * HC, (h + 1) * HC)
                hg = slice(h * HC * 4, (h + 1) * HC * 4)
                if which == 1:
                    nc.vector.quantize_mx(out=w1c[:, hc].bitcast(FP8X4), scales=w1s[:, hc], in_=w1g[:, hg])
                else:
                    nc.vector.quantize_mx(out=w2c[:, hc].bitcast(FP8X4), scales=w2s[:, hc], in_=w2g[:, hg])

            def p_q(h, t, eng):
                ts = slice(t * HC, (t + 1) * HC)
                e = nc.gpsimd if eng == "G" else nc.vector
                e.tensor_tensor(out=csq[h][:, ts], in0=dv[h][:, ts], in1=csq[h][:, ts], op=ALU.mult)

            def p_gq(h, t):
                ts = slice(t * HC, (t + 1) * HC)
                nc.tensor.matmul(out=g_p[h][:], lhsT=half_c[:], rhs=csq[h][:, ts], start=False, stop=(t == 3))

            def p_gb(h):
                nc.scalar.copy(out=g_b[:, h * HC : (h + 1) * HC], in_=g_p[h][:])

            def p_gcol():
                g_t = bank("gT", "pb")
                for jj in range(4):
                    nc.tensor.transpose(
                        out=g_t[:, jj * P : (jj + 1) * P], in_=g_b[:, jj * P : (jj + 1) * P], identity=ident[:]
                    )
                nc.vector.tensor_copy(
                    out=gcol[:].rearrange("p (j o) -> p j o", o=1),
                    in_=g_t[:].rearrange("p (j r) -> p j r", j=4)[:, :, 0:1],
                )

            glcol = pro.tile([P, 4], F32, name="glcol", tag="glcol")
            gl_b = pro.tile([P, HC], F32, name="gl_b", tag="gl_b")
            c2col = [pro.tile([P, 4], F32, name="c2col%d" % h, tag="c2col%d" % h) for h in range(2)]
            c2h = pro.tile([P, 4], F32, name="c2h", tag="c2h")
            q_a = {}

            def p_gl2(h, t):
                if t == 0:
                    g_p[h] = bank("gP", "pa")
                nc.tensor.matmul(
                    out=g_p[h][:], lhsT=half_c[:], rhs=lnr[h][:, t * HC : (t + 1) * HC], start=(t == 0), stop=(t == 3)
                )

            def p_glc():
                nc.scalar.copy(out=g_b[:, 0:HC], in_=g_p[0][:])
                g_t = bank("gT", "pa")
                for jj in range(4):
                    nc.tensor.transpose(
                        out=g_t[:, jj * P : (jj + 1) * P], in_=g_b[:, jj * P : (jj + 1) * P], identity=ident[:]
                    )
                nc.scalar.copy(
                    out=glcol[:].rearrange("p (j o) -> p j o", o=1),
                    in_=g_t[:].rearrange("p (j r) -> p j r", j=4)[:, :, 0:1],
                )

            def p_glb():
                nc.scalar.copy(out=gl_b[:], in_=g_p[1][:])

            def p_qp(h, pc, eng):
                rr = slice(pc * 256, (pc + 1) * 256)
                e = nc.gpsimd if eng == "G" else nc.vector
                e.tensor_tensor(
                    out=csq[h][:].rearrange("p (t r) -> p t r", t=4)[:, :, rr],
                    in0=dv[h][:].rearrange("p (t r) -> p t r", t=4)[:, :, rr],
                    in1=csq[h][:].rearrange("p (t r) -> p t r", t=4)[:, :, rr],
                    op=ALU.mult,
                )

            def p_at(h, jj, tag):
                if jj == 0:
                    q_a[h] = bank("qA", tag)
                for t in range(4):
                    nc.tensor.matmul(
                        out=q_a[h][:, jj * P : (jj + 1) * P],
                        lhsT=csq[h][:, t * HC + jj * P : t * HC + (jj + 1) * P],
                        rhs=ident[:],
                        is_transpose=True,
                        start=(t == 0),
                        stop=(t == 3),
                    )

            def p_c2(h):
                nc.vector.tensor_reduce(
                    out=c2col[h][:], in_=q_a[h][:].rearrange("p (j r) -> p j r", j=4), axis=AX.X, op=ALU.add
                )
                if h == 0:
                    nc.vector.scalar_tensor_tensor(
                        out=gcol[:], in0=c2col[0][:], scalar=0.5, in1=glcol[:], op0=ALU.mult, op1=ALU.add
                    )
                else:
                    nc.vector.tensor_scalar_mul(out=c2h[:], in0=c2col[1][:], scalar1=0.5)

            def p_gb2(tag):
                b_b = bank("bB", tag)
                for jj in range(4):
                    nc.tensor.transpose(
                        out=b_b[:, jj * P : (jj + 1) * P], in_=c2h[:, jj : jj + 1].to_broadcast([P, P]), identity=ident[:]
                    )
                nc.vector.tensor_tensor(out=g_b[:, HC:CLS], in0=b_b[:], in1=gl_b[:], op=ALU.add)

            p_and(0)
            p_and(1)
            p_dtr(0)
            p_rho()
            p_dtr(1)
            for h in range(2):
                for u in range(2):
                    p_ln(h, u)
            for h in range(2):
                for pr in range(2):
                    p_ctr(h, pr)
                    p_cgc(h, pr)
            p_csq(0, "V")
            for t in range(4):
                p_gl2(0, t)
            x_tr(0, 0)
            x_tr(0, 1)
            p_csq(1, "V")
            for t in range(4):
                p_gl2(1, t)
            for h in range(2):
                for pc in range(2):
                    p_exp(h, pc)
                    p_w1(h, pc, "G")
                    p_w2(h, pc)
                p_qw(h, 2)
                if h == 0:
                    p_qp(0, 0, "V")
                    p_qp(0, 1, "V")
            p_glc()
            p_glb()
            for jj in range(4):
                p_at(0, jj, "pc")
            p_qp(1, 0, "V")
            p_qp(1, 1, "V")
            x_cp(0, 0, "S")
            x_cp(0, 1, "S")
            x_tr(1, 0)
            x_tr(1, 1)
            p_c2(0)
            x_sq(0, 0, "S")
            x_sq(0, 1, "S")
            x_cp(1, 0, "S")
            x_cp(1, 1, "S")
            for jj in range(4):
                p_at(1, jj, "pc")
            x_qt(0, 0)
            p_c2(1)
            p_gb2("pc")
            p_qw(0, 1)
            p_qw(1, 1)
            x_tr(2, 0)
            x_tr(2, 1)
            x_sq(1, 0, "S")
            x_sq(1, 1, "S")
            x_cp(2, 0, "S")
            x_cp(2, 1, "S")
            x_tr(3, 0)
            x_tr(3, 1)
            x_cp(3, 0, "S")
            x_cp(3, 1, "S")
            x_sq(2, 0, "G")
            x_sq(2, 1, "G")
            x_sq(3, 0, "G")
            x_sq(3, 1, "G")
            x_qt(0, 1)
            x_qt(1, 0)
            x_qt(1, 1)
            x_qt(2, 0)
            x_qt(3, 0)

        work = ctx.enter_context(tc.tile_pool(name="work", bufs=O4_BUFS))
        stp = ctx.enter_context(tc.tile_pool(name="stp", bufs=ST_BUFS))
        o4 = {}
        s_t = {}
        pt = {}
        acc = {}
        st = {}
        dmin = {}
        nmin = {}
        sums = {}
        rec = {}

        def mx_pair(dst, l1, l1s, r1, r1s, l2, l2s, r2, r2s):
            nc.tensor.matmul_mx(
                out=dst, lhsT=l1.bitcast(FP8X4), lhsT_scale=l1s, rhs=r1.bitcast(FP8X4), rhs_scale=r1s,
                start=True, stop=False,
            )
            nc.tensor.matmul_mx(
                out=dst, lhsT=l2.bitcast(FP8X4), lhsT_scale=l2s, rhs=r2.bitcast(FP8X4), rhs_scale=r2s,
                start=False, stop=True,
            )

        def m_t(b, jj):
            if jj == 0:
                s_t[b] = stp.tile([P, 4 * 512], F32, name="s_t", tag="s_t")
            jc = slice(jj * P, (jj + 1) * P)
            pt[(b, jj)] = bank("pt", "pb")
            mx_pair(
                pt[(b, jj)][:], w1c[:, jc], w1s[:, jc], xq[b][:, 512:1024], xs[b][:, 512:1024],
                w2c[:, jc], w2s[:, jc], xq[b][:, 0:512], xs[b][:, 0:512],
            )

        def e_v(b, jj, eng):
            if eng == "S":
                nc.scalar.activation(
                    out=s_t[b][:, jj * 512 : (jj + 1) * 512], in_=pt[(b, jj)][:], func=ACT.Identity,
                    bias=gcol[:, jj : jj + 1], scale=1.0,
                )
            else:
                nc.vector.tensor_scalar_add(
                    out=s_t[b][:, jj * 512 : (jj + 1) * 512], in0=pt[(b, jj)][:], scalar1=gcol[:, jj : jj + 1]
                )

        def m_d(b, i):
            if i == 0:
                o4[b] = work.tile([P, 4 * CLS], F32, name="o4", tag="o4")
            rc = slice(i * P, (i + 1) * P)
            rc2 = slice(512 + i * P, 512 + (i + 1) * P)
            hc = slice(HC, CLS)
            acc[(b, i)] = bank("acc", "pc")
            mx_pair(
                acc[(b, i)][:], xq[b][:, rc2], xs[b][:, rc2], w1c[:, hc], w1s[:, hc],
                xq[b][:, rc], xs[b][:, rc], w2c[:, hc], w2s[:, hc],
            )

        def a_d(b, i):
            nc.vector.tensor_tensor(
                out=o4[b][:, i * CLS + HC : (i + 1) * CLS], in0=acc[(b, i)][:], in1=g_b[:, HC:CLS], op=ALU.add
            )

        def d_m(b):
            dmin[b] = small.tile([P, 4], F32, name="dmin", tag="dmin")
            nmin[b] = small.tile([P, 4], F32, name="nmin", tag="nmin")
            nc.vector.tensor_reduce(
                out=dmin[b][:], in_=o4[b][:].rearrange("p (i k) -> p i k", i=4)[:, :, HC:CLS], axis=AX.X, op=ALU.min
            )

        def b_t(b, i):
            st[(b, i)] = bank("st", "pa")
            for jj in range(4):
                nc.tensor.transpose(
                    out=st[(b, i)][:, jj * P : (jj + 1) * P],
                    in_=s_t[b][:, jj * 512 + i * P : jj * 512 + (i + 1) * P],
                    identity=ident[:],
                )

        def e_m(b, i):
            nc.vector.tensor_scalar(
                out=o4[b][:, i * CLS : i * CLS + HC], in0=st[(b, i)][:], scalar1=0.0, scalar2=dmin[b][:, i : i + 1],
                op0=ALU.add, op1=ALU.min, accum_out=nmin[b][:, i : i + 1],
            )

        def e_x(b, i):
            if i == 0:
                sums[b] = small.tile([P, 4], F32, name="sums", tag="sums")
                rec[b] = small.tile([P, 4], F32, name="rec", tag="rec")
            ic = slice(i * CLS, (i + 1) * CLS)
            nc.scalar.activation(
                out=o4[b][:, ic], in_=o4[b][:, ic], func=ACT.Exp, bias=nmin[b][:, i : i + 1], scale=-1.0,
                accum_out=sums[b][:, i : i + 1],
            )

        def r_c(b):
            nc.vector.reciprocal(out=rec[b][:], in_=sums[b][:])

        def r_c1(b, i):
            nc.vector.reciprocal(out=rec[b][:, i : i + 1], in_=sums[b][:, i : i + 1])

        def s_c(b, i, eng="G"):
            ic = slice(i * CLS, (i + 1) * CLS)
            if eng == "V":
                nc.vector.tensor_scalar_mul(
                    out=o4[b][:, ic], in0=o4[b][:, ic], scalar1=rec[b][:, i : i + 1]
                )
            else:
                nc.gpsimd.tensor_scalar(
                    out=o4[b][:, ic], in0=o4[b][:, ic], scalar1=rec[b][:, i : i + 1], scalar2=0.0,
                    op0=ALU.mult, op1=ALU.add,
                )

        def store1(b, i):
            nc.sync.dma_start(out=out_v[:, 4 * b + i, :], in_=o4[b][:, i * CLS : (i + 1) * CLS])

        def s_t_ore(b, pr):
            t0 = 4 * b + 2 * pr
            nc.sync.dma_start(
                out=out_v[:, t0 : t0 + 2, :],
                in_=o4[b][:].rearrange("p (i k) -> p i k", i=4)[:, 2 * pr : 2 * pr + 2, :],
            )

        def sched(n):
            todo = {}
            for key in OFF:
                m = n - OFF[key]
                todo[key] = (m // 4, m % 4) if 0 <= m < 4 * NB else None
            return todo

        for n in range(N_LO, 4 * NB + N_HI + 1):
            td = sched(n)
            if td["bt"]:
                b_t(*td["bt"])
            if td["xtr"] and td["xtr"][1] % 2 == 0 and td["xtr"][0] >= PRE:
                x_tr(td["xtr"][0], td["xtr"][1] // 2)
            if td["mt"]:
                m_t(*td["mt"])
            if td["md"]:
                m_d(*td["md"])
            if td["em"]:
                e_m(*td["em"])
            if td["ev"]:
                e_v(td["ev"][0], td["ev"][1], "S")
            if td["ad"]:
                a_d(*td["ad"])
                if td["ad"][1] == 3:
                    d_m(td["ad"][0])
            if td["ex"]:
                e_x(*td["ex"])
            if td["xcp"] and td["xcp"][1] % 2 == 0 and td["xcp"][0] >= PRE:
                x_cp(td["xcp"][0], td["xcp"][1] // 2, "S")
            if td["xq0"] and td["xq0"][1] == 0 and td["xq0"][0] >= PRE:
                x_qt(td["xq0"][0], 0)
            if td["rc"] and td["rc"][0] >= NB - LASTV:
                r_c1(*td["rc"])
                s_c(td["rc"][0], td["rc"][1], "V")
                store1(*td["rc"])
            elif td["rc"] and td["rc"][1] == 3:
                r_c(td["rc"][0])
            if td["sc"] and td["sc"][0] < NB - LASTV:
                s_c(*td["sc"])
                if td["sc"][0] >= NB - LAST1:
                    store1(*td["sc"])
                elif td["sc"][1] % 2 == 1:
                    s_t_ore(td["sc"][0], td["sc"][1] // 2)
            if td["xsq"] and td["xsq"][1] % 2 == 0 and td["xsq"][0] >= PRE:
                x_sq(td["xsq"][0], td["xsq"][1] // 2, SQM[td["xsq"][0]][td["xsq"][1] // 2])
            if td["xq1"] and td["xq1"][1] == 0 and td["xq1"][0] >= PRE_Q1:
                x_qt(td["xq1"][0], 1)
